import numpy as np
import ml_dtypes


def mxq(x, axis, fmt="e4m3"):
    dtype, down = {"e4m3": (ml_dtypes.float8_e4m3fn, 7), "e5m2": (ml_dtypes.float8_e5m2, 14)}[fmt]
    v = np.moveaxis(np.asarray(x, np.float32).astype(ml_dtypes.bfloat16).astype(np.float64), axis, -1)
    blocks = v.reshape(v.shape[:-1] + (-1, 32))
    amax = np.abs(blocks).max(-1, keepdims=True)
    byte = np.maximum(np.where(amax > 0, np.frexp(amax)[1] - 1 + 127, 0) - down, 1)
    scale = np.exp2(byte - 127.0)
    codes = (blocks / scale).astype(np.float32).astype(dtype).astype(np.float64)
    return np.moveaxis((codes * scale).reshape(v.shape), -1, axis)


WIDE = False


def mx_kscale(k):
    if not WIDE:
        return np.ones(k)
    levels = np.array([10, -10, 5, -5, 0])
    a = np.random.permutation(np.resize(levels, k // 512 * 4)).reshape(k // 512, 4)
    idx = np.arange(k)
    return np.exp2(a[idx // 512, idx % 128 // 32])


BF16 = ml_dtypes.bfloat16


def bf(x):
    return np.asarray(x, np.float32).astype(BF16)


def f64(x):
    return np.asarray(x).astype(np.float64)


E2M1 = np.array([0.0, 0.5, 1.0, 1.5, 2.0, 3.0, 4.0, 6.0, -0.0, -0.5, -1.0, -1.5, -2.0, -3.0, -4.0, -6.0])


def pack_weight(w, fmt):
    k, n = w.shape
    w = f64(bf(w)).reshape(k // 32, 32, n)
    amax = np.abs(w).max(1)
    if fmt == "e4m3":
        byte = np.frexp(amax)[1] - 1 + 127 - 7
    else:
        mant, ex = np.frexp(amax / 6.0)
        byte = np.where(mant > 0.5, ex, ex - 1) + 127
    byte = np.clip(np.where(amax > 0, byte, 1), 1, 254)
    scaled = (w * np.exp2(127.0 - byte)[:, None, :]).reshape(k, n).astype(np.float32)
    by_word = np.ascontiguousarray(scaled.reshape(k // 512, 128, 4, n).transpose(0, 1, 3, 2))
    if fmt == "e4m3":
        words = by_word.astype(ml_dtypes.float8_e4m3fn).view(np.uint8)
    else:
        c = by_word.astype(ml_dtypes.float4_e2m1fn).view(np.uint8) & 0xF
        words = c[..., 0::2] | (c[..., 1::2] << 4)
    return np.ascontiguousarray(words), np.ascontiguousarray(byte.astype(np.uint8).reshape(k // 512, 16, n))


def unpack_weight(words, scales, fmt):
    g, p, n, _ = words.shape
    if fmt == "e4m3":
        vals = np.ascontiguousarray(words).view(ml_dtypes.float8_e4m3fn).astype(np.float64)
    else:
        nib = np.empty((g, p, n, 4), np.uint8)
        nib[..., 0::2] = words & 0xF
        nib[..., 1::2] = words >> 4
        vals = E2M1[nib]
    vals = vals * np.repeat(np.exp2(scales.astype(np.float64) - 127.0), 8, axis=1)[..., None]
    return vals.transpose(0, 1, 3, 2).reshape(g * 512, n)


B, S, D, R, C = 128, 32, 512, 16, 1024
MIN_SCALE = 1e-3
TEMPERATURE = 1.5
FMT = "e4m3"


def softplus(v):
    return np.logaddexp(v, 0.0)


def setup_inputs():
    s = mx_kscale(D)
    features = bf(np.random.standard_normal((B, D)) * 0.3 * s)
    W_diag_words, W_diag_scales = pack_weight((np.random.standard_normal((D, D)) * 2.0 / np.sqrt(D) / s[None, :]).T, FMT)
    b_diag = bf(-4.0 + 0.2 * np.random.standard_normal(D))
    W_cls_words, W_cls_scales = pack_weight((np.random.standard_normal((C, D)) * 3.0 / np.sqrt(D) / s[None, :]).T, FMT)
    b_cls = bf(np.random.standard_normal(C) * 0.3)
    noise_diag = bf(np.random.standard_normal((B, S, D)) * 10.0 * s)
    lr_samples = bf(np.random.standard_normal((B, S, D)) * 0.3 * s)
    return {
        "features": features,
        "W_diag_words": W_diag_words,
        "W_diag_scales": W_diag_scales,
        "b_diag": b_diag,
        "W_cls_words": W_cls_words,
        "W_cls_scales": W_cls_scales,
        "b_cls": b_cls,
        "noise_diag": noise_diag,
        "lr_samples": lr_samples,
    }


def reference(features, W_diag_words, W_diag_scales, b_diag, W_cls_words, W_cls_scales, b_cls, noise_diag, lr_samples):
    f = f64(features)
    z = (mxq(f, 1, "e4m3") @ unpack_weight(W_diag_words, W_diag_scales, FMT)) + f64(b_diag)
    diagonal_std = softplus(z) + MIN_SCALE
    samples = f64(lr_samples) + diagonal_std[:, None, :] * f64(noise_diag)
    pre_logits = f[:, None, :] + samples
    logits = (mxq(pre_logits, 2, "e4m3") @ unpack_weight(W_cls_words, W_cls_scales, FMT)) + f64(b_cls)
    return logits / TEMPERATURE

@@ -1,0 +1,221 @@
+from contextlib import ExitStack
+
+import concourse.mybir as mybir
+from concourse.masks import make_identity
+
+F32 = mybir.dt.float32
+BF16 = mybir.dt.bfloat16
+I32 = mybir.dt.int32
+U32 = mybir.dt.uint32
+U8 = mybir.dt.uint8
+FP8X4 = mybir.dt.float8_e4m3fn_x4
+ACT = mybir.ActivationFunctionType
+ALU = mybir.AluOpType
+
+B, S, D, C = 128, 32, 512, 1024
+MIN_SCALE = 1e-3
+INV_TEMPERATURE = 1.0 / 1.5
+
+P = 128
+PACK = 4
+HALVES = 2
+ROWS_PER_Q = 2
+GROUP_ROWS = P * ROWS_PER_Q
+GROUPS = B * S // GROUP_ROWS
+B_PER_GROUP = GROUP_ROWS // S
+Q_PER_B = P // B_PER_GROUP
+N_TILE = 512
+LOAD_GROUPS = 2
+
+FLOPS = 2 * B * D * D + 2 * B * S * D * C
+
+
+def load_weight(nc, words, plane, words_dram, scales_dram):
+    nc.vector.memset(plane[:].bitcast(I32), 0)
+    scale_rows = scales_dram.rearrange("g q n -> (g q) n").bitcast(I32)
+    for r in range(4):
+        nc.sync.dma_start(out=plane[r:P:32, :].bitcast(I32), in_=scale_rows[r:16:4, :])
+    nc.sync.dma_start(
+        out=words[:].bitcast(I32),
+        in_=words_dram.rearrange("g p n t -> (g p) (n t)").bitcast(I32),
+    )
+
+
+def tile_hetxlhead_pa_kernel(
+    tc, features, W_diag_words, W_diag_scales, b_diag, W_cls_words, W_cls_scales, b_cls, noise_diag, lr_samples, out
+):
+    nc = tc.nc
+    noise_rows = noise_diag.flatten_outer_dims().rearrange("(g q sl) d -> q g (sl d)", q=P, sl=ROWS_PER_Q)
+    lr_rows = lr_samples.flatten_outer_dims().rearrange("(g q sl) d -> q g (sl d)", q=P, sl=ROWS_PER_Q)
+    out_rows = out.flatten_outer_dims().rearrange("(g q sl) c -> q g (sl c)", q=P, sl=ROWS_PER_Q)
+
+    with ExitStack() as stack:
+        keep = stack.enter_context(tc.tile_pool(name="keep", bufs=1))
+        work = stack.enter_context(tc.tile_pool(name="work", bufs=3))
+        store = stack.enter_context(tc.tile_pool(name="store", bufs=4))
+        flipped = stack.enter_context(tc.psum_pool(name="flipped", bufs=2))
+        sums = stack.enter_context(tc.psum_pool(name="sums", bufs=4))
+
+        f_sb = keep.tile([P, D], BF16)
+        nc.sync.dma_start(out=f_sb[:], in_=features)
+        wd_words = keep.tile([P, D], U32, align_bytes=64)
+        wd_plane = keep.tile([P, D], U8, align_bytes=64)
+        load_weight(nc, wd_words, wd_plane, W_diag_words, W_diag_scales)
+        bdiag_all = keep.tile([P, D], BF16)
+        nc.scalar.dma_start(out=bdiag_all[:], in_=b_diag.partition_broadcast(P))
+        bcls_all = keep.tile([P, C], BF16)
+        nc.scalar.dma_start(out=bcls_all[:], in_=b_cls.partition_broadcast(P))
+
+        noise_sb = keep.tile([P, GROUPS, ROWS_PER_Q * D], BF16)
+        lr_sb = keep.tile([P, GROUPS, ROWS_PER_Q * D], BF16)
+        wc_words = keep.tile([P, C], U32, align_bytes=64)
+        wc_plane = keep.tile([P, C], U8, align_bytes=64)
+        for g0 in range(0, GROUPS, LOAD_GROUPS):
+            some = slice(g0, g0 + LOAD_GROUPS)
+            nc.sync.dma_start(out=noise_sb[:, some, :], in_=noise_rows[:, some, :])
+            nc.sync.dma_start(out=lr_sb[:, some, :], in_=lr_rows[:, some, :])
+            if g0 == 0:
+                load_weight(nc, wc_words, wc_plane, W_cls_words, W_cls_scales)
+
+        ident = keep.tile([P, P], F32)
+        make_identity(nc, ident[:])
+        one = keep.tile([P, 1], F32)
+        nc.vector.memset(one[:], 1.0)
+
+        def flip_words(dst, rows_bf16, first_word):
+            words = rows_bf16.bitcast(F32)
+            for u in range(HALVES):
+                nc.tensor.transpose(
+                    out=dst[u],
+                    in_=words[:, first_word + u : first_word + D // 2 : HALVES],
+                    identity=ident[:],
+                )
+
+        fT_ps = flipped.tile([P, HALVES, P], F32, tag="noiseT")
+        flip_words([fT_ps[:, u, :] for u in range(HALVES)], f_sb[:], 0)
+        f_grouped = keep.tile([P, B, PACK], BF16, align_bytes=64)
+        nc.vector.tensor_copy(
+            out=f_grouped[:].rearrange("p b t -> p (b t)").bitcast(F32).rearrange("p (b u) -> p b u", u=HALVES),
+            in_=fT_ps[:].rearrange("p u b -> p b u"),
+        )
+        f_codes = keep.tile([P, B], U32, align_bytes=64)
+        f_scales = keep.tile([P, B], U8, align_bytes=64)
+        nc.vector.quantize_mx(
+            out=f_codes[:].bitcast(FP8X4), scales=f_scales[:], in_=f_grouped[:].rearrange("p b t -> p (b t)")
+        )
+        fT = keep.tile([P, PACK, B], F32)
+        nc.scalar.copy(out=fT[:], in_=f_grouped[:].rearrange("p b t -> p t b"))
+
+        z_ps = sums.tile([P, D], F32, tag="acc")
+        nc.tensor.matmul_mx(
+            out=z_ps[:],
+            lhsT=f_codes[:].bitcast(FP8X4),
+            lhsT_scale=f_scales[:],
+            rhs=wd_words[:].bitcast(FP8X4),
+            rhs_scale=wd_plane[:],
+            start=True,
+            stop=True,
+        )
+        z = keep.tile([P, D], F32)
+        nc.vector.tensor_tensor(out=z[:], in0=z_ps[:], in1=bdiag_all[:], op=ALU.add)
+        tail = keep.tile([P, D], F32)
+        nc.scalar.activation(out=tail[:], in_=z[:], func=ACT.Abs)
+        nc.scalar.activation(out=tail[:], in_=tail[:], func=ACT.Exp, scale=-1.0)
+        nc.scalar.activation(out=tail[:], in_=tail[:], func=ACT.Ln, bias=one[:])
+        ramp = keep.tile([P, D], F32)
+        nc.vector.tensor_scalar(out=ramp[:], in0=z[:], scalar1=0.0, scalar2=MIN_SCALE, op0=ALU.max, op1=ALU.add)
+        std_sorted = keep.tile([P, PACK, P], F32)
+        nc.vector.tensor_tensor(
+            out=std_sorted[:],
+            in0=ramp[:].rearrange("b (p t) -> b t p", t=PACK),
+            in1=tail[:].rearrange("b (p t) -> b t p", t=PACK),
+            op=ALU.add,
+        )
+        stdT_ps = flipped.tile([P, PACK, B], F32, tag="lrT")
+        for t in range(PACK):
+            nc.tensor.transpose(out=stdT_ps[:, t, :], in_=std_sorted[:, t, :], identity=ident[:])
+        stdT = keep.tile([P, PACK, B], F32)
+        nc.vector.tensor_copy(out=stdT[:], in_=stdT_ps[:])
+
+        bias_scaled = keep.tile([P, C], F32)
+        nc.vector.tensor_scalar(
+            out=bias_scaled[:], in0=bcls_all[:], scalar1=INV_TEMPERATURE, scalar2=None, op0=ALU.mult
+        )
+
+        def as_pairs(bank):
+            flat = bank[:].rearrange("p u sl q -> p (u sl q)").bitcast(BF16)
+            return flat.rearrange("p (u r e) -> p u r e", u=HALVES, e=2)
+
+        def flip_group(g):
+            noiseT = flipped.tile([P, HALVES, ROWS_PER_Q, P], F32, tag="noiseT")
+            lrT = flipped.tile([P, HALVES, ROWS_PER_Q, P], F32, tag="lrT")
+            for bank, rows in ((noiseT, noise_sb), (lrT, lr_sb)):
+                for sl in range(ROWS_PER_Q):
+                    flip_words([bank[:, u, sl, :] for u in range(HALVES)], rows[:, g, :], sl * (D // 2))
+            return noiseT, lrT
+
+        def scale_noise(g, noiseT):
+            scaled = work.tile([P, PACK, ROWS_PER_Q, P], F32)
+            pairs = as_pairs(noiseT).rearrange("p u (sl q) e -> p u sl q e", sl=ROWS_PER_Q)
+            for i in range(B_PER_GROUP):
+                b = g * B_PER_GROUP + i
+                its_q = slice(i * Q_PER_B, (i + 1) * Q_PER_B)
+                for t in range(PACK):
+                    nc.scalar.activation(
+                        out=scaled[:, t, :, its_q],
+                        in_=pairs[:, t // 2, :, its_q, t % 2],
+                        func=ACT.Identity,
+                        scale=stdT[:, t, b : b + 1],
+                        bias=fT[:, t, b : b + 1],
+                    )
+            return scaled
+
+        def add_and_quantise(scaled, lrT):
+            pre = work.tile([P, GROUP_ROWS, PACK], BF16, align_bytes=64)
+            nc.vector.tensor_tensor(
+                out=pre[:].rearrange("p r (u e) -> p r u e", u=HALVES),
+                in0=scaled[:].rearrange("p (u e) sl q -> p (sl q) u e", u=HALVES),
+                in1=as_pairs(lrT).rearrange("p u r e -> p r u e"),
+                op=ALU.add,
+            )
+            codes = work.tile([P, GROUP_ROWS], U32, align_bytes=64)
+            scales = work.tile([P, GROUP_ROWS], U8, align_bytes=64)
+            nc.vector.quantize_mx(
+                out=codes[:].bitcast(FP8X4), scales=scales[:], in_=pre[:].rearrange("p r t -> p (r t)")
+            )
+            return codes, scales
+
+        def classify(g, codes, scales):
+            logits = store.tile([P, ROWS_PER_Q, C], F32)
+            for sl in range(ROWS_PER_Q):
+                its_rows = slice(sl * P, (sl + 1) * P)
+                for n0 in range(0, C, N_TILE):
+                    its_classes = slice(n0, n0 + N_TILE)
+                    acc = sums.tile([P, N_TILE], F32, tag="acc")
+                    nc.tensor.matmul_mx(
+                        out=acc[:],
+                        lhsT=codes[:, its_rows].bitcast(FP8X4),
+                        lhsT_scale=scales[:, its_rows],
+                        rhs=wc_words[:, its_classes].bitcast(FP8X4),
+                        rhs_scale=wc_plane[:, its_classes],
+                        start=True,
+                        stop=True,
+                    )
+                    nc.vector.scalar_tensor_tensor(
+                        out=logits[:, sl, its_classes],
+                        in0=acc[:],
+                        scalar=INV_TEMPERATURE,
+                        in1=bias_scaled[:, its_classes],
+                        op0=ALU.mult,
+                        op1=ALU.add,
+                    )
+            nc.sync.dma_start(out=out_rows[:, g, :], in_=logits[:].rearrange("q sl c -> q (sl c)"))
+
+        banks = {0: flip_group(0)}
+        for g in range(GROUPS):
+            if g + 1 < GROUPS:
+                banks[g + 1] = flip_group(g + 1)
+            noiseT, lrT = banks[g]
+            scaled = scale_noise(g, noiseT)
+            codes, scales = add_and_quantise(scaled, lrT)
+            classify(g, codes, scales)

@@ -55,6 +55,7 @@ def tile_hetxlhead_pa_kernel(
         store = stack.enter_context(tc.tile_pool(name="store", bufs=4))
         flipped = stack.enter_context(tc.psum_pool(name="flipped", bufs=2))
         sums = stack.enter_context(tc.psum_pool(name="sums", bufs=4))
+        stack.enter_context(tc.manual_schedule())
 
         f_sb = keep.tile([P, D], BF16)
         nc.sync.dma_start(out=f_sb[:], in_=features)
@@ -81,6 +82,8 @@ def tile_hetxlhead_pa_kernel(
         make_identity(nc, ident[:])
         one = keep.tile([P, 1], F32)
         nc.vector.memset(one[:], 1.0)
+        warm = keep.tile([P, 1], F32)
+        nc.scalar.activation(out=warm[:], in_=one[:], func=ACT.Exp)
 
         def flip_words(dst, rows_bf16, first_word):
             words = rows_bf16.bitcast(F32)
@@ -91,13 +94,94 @@ def tile_hetxlhead_pa_kernel(
                     identity=ident[:],
                 )
 
-        fT_ps = flipped.tile([P, HALVES, P], F32, tag="noiseT")
+        def interleave(grouped, bank_words):
+            dst = grouped[:].rearrange("p r t -> p (r t)").bitcast(F32).rearrange("p (r u) -> p r u", u=HALVES)
+            return dst, bank_words.rearrange("p u r -> p r u")
+
+        def flip_group(g):
+            noiseT = flipped.tile([P, HALVES, ROWS_PER_Q, P], F32, tag="noiseT")
+            lrT = flipped.tile([P, HALVES, ROWS_PER_Q, P], F32, tag="lrT")
+            for bank, rows in ((noiseT, noise_sb), (lrT, lr_sb)):
+                for sl in range(ROWS_PER_Q):
+                    flip_words([bank[:, u, sl, :] for u in range(HALVES)], rows[:, g, :], sl * (D // 2))
+            return noiseT, lrT
+
+        def scale_noise(g, noiseT, lrT):
+            lr_grouped = work.tile([P, GROUP_ROWS, PACK], BF16)
+            dst, src = interleave(lr_grouped, lrT[:].rearrange("p u sl q -> p u (sl q)"))
+            nc.scalar.copy(out=dst, in_=src)
+            scaled = work.tile([P, PACK, ROWS_PER_Q, P], F32)
+            pairs = (
+                noiseT[:]
+                .rearrange("p u sl q -> p (u sl q)")
+                .bitcast(BF16)
+                .rearrange("p (u sl q e) -> p u sl q e", u=HALVES, sl=ROWS_PER_Q, e=2)
+            )
+            for i in range(B_PER_GROUP):
+                b = g * B_PER_GROUP + i
+                its_q = slice(i * Q_PER_B, (i + 1) * Q_PER_B)
+                for t in range(PACK):
+                    nc.scalar.activation(
+                        out=scaled[:, t, :, its_q],
+                        in_=pairs[:, t // 2, :, its_q, t % 2],
+                        func=ACT.Identity,
+                        scale=stdT[:, t, b : b + 1],
+                        bias=fT[:, t, b : b + 1],
+                    )
+            return scaled, lr_grouped
+
+        def add_lr(scaled, lr_grouped):
+            pre = work.tile([P, GROUP_ROWS, PACK], BF16, align_bytes=64)
+            nc.gpsimd.tensor_tensor(
+                out=pre[:], in0=scaled[:].rearrange("p t sl q -> p (sl q) t"), in1=lr_grouped[:], op=ALU.add
+            )
+            return pre
+
+        def quantise(pre):
+            codes = work.tile([P, GROUP_ROWS], U32, align_bytes=64)
+            scales = work.tile([P, GROUP_ROWS], U8, align_bytes=64)
+            nc.vector.quantize_mx(
+                out=codes[:].bitcast(FP8X4), scales=scales[:], in_=pre[:].rearrange("p r t -> p (r t)")
+            )
+            return codes, scales
+
+        def multiply(codes, scales):
+            parts = []
+            for sl in range(ROWS_PER_Q):
+                its_rows = slice(sl * P, (sl + 1) * P)
+                for n0 in range(0, C, N_TILE):
+                    its_classes = slice(n0, n0 + N_TILE)
+                    acc = sums.tile([P, N_TILE], F32, tag="acc")
+                    nc.tensor.matmul_mx(
+                        out=acc[:],
+                        lhsT=codes[:, its_rows].bitcast(FP8X4),
+                        lhsT_scale=scales[:, its_rows],
+                        rhs=wc_words[:, its_classes].bitcast(FP8X4),
+                        rhs_scale=wc_plane[:, its_classes],
+                        start=True,
+                        stop=True,
+                    )
+                    parts.append((sl, its_classes, acc))
+            return parts
+
+        def finish(g, parts):
+            logits = store.tile([P, ROWS_PER_Q, C], F32)
+            for sl, its_classes, acc in parts:
+                nc.vector.scalar_tensor_tensor(
+                    out=logits[:, sl, its_classes],
+                    in0=acc[:],
+                    scalar=INV_TEMPERATURE,
+                    in1=bias_scaled[:, its_classes],
+                    op0=ALU.mult,
+                    op1=ALU.add,
+                )
+            nc.sync.dma_start(out=out_rows[:, g, :], in_=logits[:].rearrange("q sl c -> q (sl c)"))
+
+        fT_ps = sums.tile([P, HALVES, B], F32, tag="acc")
         flip_words([fT_ps[:, u, :] for u in range(HALVES)], f_sb[:], 0)
         f_grouped = keep.tile([P, B, PACK], BF16, align_bytes=64)
-        nc.vector.tensor_copy(
-            out=f_grouped[:].rearrange("p b t -> p (b t)").bitcast(F32).rearrange("p (b u) -> p b u", u=HALVES),
-            in_=fT_ps[:].rearrange("p u b -> p b u"),
-        )
+        dst, src = interleave(f_grouped, fT_ps[:])
+        nc.vector.tensor_copy(out=dst, in_=src)
         f_codes = keep.tile([P, B], U32, align_bytes=64)
         f_scales = keep.tile([P, B], U8, align_bytes=64)
         nc.vector.quantize_mx(
@@ -116,6 +200,7 @@ def tile_hetxlhead_pa_kernel(
             start=True,
             stop=True,
         )
+        banks = {0: flip_group(0), 1: flip_group(1)}
         z = keep.tile([P, D], F32)
         nc.vector.tensor_tensor(out=z[:], in0=z_ps[:], in1=bdiag_all[:], op=ALU.add)
         tail = keep.tile([P, D], F32)
@@ -131,91 +216,28 @@ def tile_hetxlhead_pa_kernel(
             in1=tail[:].rearrange("b (p t) -> b t p", t=PACK),
             op=ALU.add,
         )
-        stdT_ps = flipped.tile([P, PACK, B], F32, tag="lrT")
+        stdT_ps = sums.tile([P, PACK, B], F32, tag="acc")
         for t in range(PACK):
             nc.tensor.transpose(out=stdT_ps[:, t, :], in_=std_sorted[:, t, :], identity=ident[:])
         stdT = keep.tile([P, PACK, B], F32)
         nc.vector.tensor_copy(out=stdT[:], in_=stdT_ps[:])
-
         bias_scaled = keep.tile([P, C], F32)
         nc.vector.tensor_scalar(
             out=bias_scaled[:], in0=bcls_all[:], scalar1=INV_TEMPERATURE, scalar2=None, op0=ALU.mult
         )
 
-        def as_pairs(bank):
-            flat = bank[:].rearrange("p u sl q -> p (u sl q)").bitcast(BF16)
-            return flat.rearrange("p (u r e) -> p u r e", u=HALVES, e=2)
-
-        def flip_group(g):
-            noiseT = flipped.tile([P, HALVES, ROWS_PER_Q, P], F32, tag="noiseT")
-            lrT = flipped.tile([P, HALVES, ROWS_PER_Q, P], F32, tag="lrT")
-            for bank, rows in ((noiseT, noise_sb), (lrT, lr_sb)):
-                for sl in range(ROWS_PER_Q):
-                    flip_words([bank[:, u, sl, :] for u in range(HALVES)], rows[:, g, :], sl * (D // 2))
-            return noiseT, lrT
-
-        def scale_noise(g, noiseT):
-            scaled = work.tile([P, PACK, ROWS_PER_Q, P], F32)
-            pairs = as_pairs(noiseT).rearrange("p u (sl q) e -> p u sl q e", sl=ROWS_PER_Q)
-            for i in range(B_PER_GROUP):
-                b = g * B_PER_GROUP + i
-                its_q = slice(i * Q_PER_B, (i + 1) * Q_PER_B)
-                for t in range(PACK):
-                    nc.scalar.activation(
-                        out=scaled[:, t, :, its_q],
-                        in_=pairs[:, t // 2, :, its_q, t % 2],
-                        func=ACT.Identity,
-                        scale=stdT[:, t, b : b + 1],
-                        bias=fT[:, t, b : b + 1],
-                    )
-            return scaled
-
-        def add_and_quantise(scaled, lrT):
-            pre = work.tile([P, GROUP_ROWS, PACK], BF16, align_bytes=64)
-            nc.vector.tensor_tensor(
-                out=pre[:].rearrange("p r (u e) -> p r u e", u=HALVES),
-                in0=scaled[:].rearrange("p (u e) sl q -> p (sl q) u e", u=HALVES),
-                in1=as_pairs(lrT).rearrange("p u r e -> p r u e"),
-                op=ALU.add,
-            )
-            codes = work.tile([P, GROUP_ROWS], U32, align_bytes=64)
-            scales = work.tile([P, GROUP_ROWS], U8, align_bytes=64)
-            nc.vector.quantize_mx(
-                out=codes[:].bitcast(FP8X4), scales=scales[:], in_=pre[:].rearrange("p r t -> p (r t)")
-            )
-            return codes, scales
-
-        def classify(g, codes, scales):
-            logits = store.tile([P, ROWS_PER_Q, C], F32)
-            for sl in range(ROWS_PER_Q):
-                its_rows = slice(sl * P, (sl + 1) * P)
-                for n0 in range(0, C, N_TILE):
-                    its_classes = slice(n0, n0 + N_TILE)
-                    acc = sums.tile([P, N_TILE], F32, tag="acc")
-                    nc.tensor.matmul_mx(
-                        out=acc[:],
-                        lhsT=codes[:, its_rows].bitcast(FP8X4),
-                        lhsT_scale=scales[:, its_rows],
-                        rhs=wc_words[:, its_classes].bitcast(FP8X4),
-                        rhs_scale=wc_plane[:, its_classes],
-                        start=True,
-                        stop=True,
-                    )
-                    nc.vector.scalar_tensor_tensor(
-                        out=logits[:, sl, its_classes],
-                        in0=acc[:],
-                        scalar=INV_TEMPERATURE,
-                        in1=bias_scaled[:, its_classes],
-                        op0=ALU.mult,
-                        op1=ALU.add,
-                    )
-            nc.sync.dma_start(out=out_rows[:, g, :], in_=logits[:].rearrange("q sl c -> q (sl c)"))
-
-        banks = {0: flip_group(0)}
-        for g in range(GROUPS):
-            if g + 1 < GROUPS:
-                banks[g + 1] = flip_group(g + 1)
-            noiseT, lrT = banks[g]
-            scaled = scale_noise(g, noiseT)
-            codes, scales = add_and_quantise(scaled, lrT)
-            classify(g, codes, scales)
+        pres = {}
+        accs = {}
+        for g in range(GROUPS + 2):
+            if g < GROUPS:
+                noiseT, lrT = banks[g]
+                scaled, lr_grouped = scale_noise(g, noiseT, lrT)
+                pres[g] = add_lr(scaled, lr_grouped)
+            if 1 <= g <= GROUPS:
+                codes, scales = quantise(pres[g - 1])
+            if g >= 2:
+                finish(g - 2, accs[g - 2])
+            if 1 <= g <= GROUPS:
+                accs[g - 1] = multiply(codes, scales)
+            if g + 2 < GROUPS:
+                banks[g + 2] = flip_group(g + 2)

@@ -26,6 +26,7 @@ B_PER_GROUP = GROUP_ROWS // S
 Q_PER_B = P // B_PER_GROUP
 N_TILE = 512
 LOAD_GROUPS = 2
+VECTOR_COPIES = 6
 
 FLOPS = 2 * B * D * D + 2 * B * S * D * C
 
@@ -47,25 +48,25 @@ def tile_hetxlhead_pa_kernel(
     nc = tc.nc
     noise_rows = noise_diag.flatten_outer_dims().rearrange("(g q sl) d -> q g (sl d)", q=P, sl=ROWS_PER_Q)
     lr_rows = lr_samples.flatten_outer_dims().rearrange("(g q sl) d -> q g (sl d)", q=P, sl=ROWS_PER_Q)
-    out_rows = out.flatten_outer_dims().rearrange("(g q sl) c -> q g (sl c)", q=P, sl=ROWS_PER_Q)
+    out_rows = out.flatten_outer_dims().rearrange("(g q sl) c -> q g sl c", q=P, sl=ROWS_PER_Q)
 
     with ExitStack() as stack:
         keep = stack.enter_context(tc.tile_pool(name="keep", bufs=1))
         work = stack.enter_context(tc.tile_pool(name="work", bufs=3))
-        store = stack.enter_context(tc.tile_pool(name="store", bufs=4))
+        store = stack.enter_context(tc.tile_pool(name="store", bufs=6))
         flipped = stack.enter_context(tc.psum_pool(name="flipped", bufs=2))
         sums = stack.enter_context(tc.psum_pool(name="sums", bufs=4))
         stack.enter_context(tc.manual_schedule())
 
         f_sb = keep.tile([P, D], BF16)
         nc.sync.dma_start(out=f_sb[:], in_=features)
+        bias_rows = keep.tile([P, D + C], BF16)
+        nc.vector.memset(bias_rows[:].bitcast(I32), 0)
+        nc.sync.dma_start(out=bias_rows[0:1, 0:D], in_=b_diag.unsqueeze(0))
+        nc.sync.dma_start(out=bias_rows[0:1, D : D + C], in_=b_cls.unsqueeze(0))
         wd_words = keep.tile([P, D], U32, align_bytes=64)
         wd_plane = keep.tile([P, D], U8, align_bytes=64)
         load_weight(nc, wd_words, wd_plane, W_diag_words, W_diag_scales)
-        bdiag_all = keep.tile([P, D], BF16)
-        nc.scalar.dma_start(out=bdiag_all[:], in_=b_diag.partition_broadcast(P))
-        bcls_all = keep.tile([P, C], BF16)
-        nc.scalar.dma_start(out=bcls_all[:], in_=b_cls.partition_broadcast(P))
 
         noise_sb = keep.tile([P, GROUPS, ROWS_PER_Q * D], BF16)
         lr_sb = keep.tile([P, GROUPS, ROWS_PER_Q * D], BF16)
@@ -75,15 +76,20 @@ def tile_hetxlhead_pa_kernel(
             some = slice(g0, g0 + LOAD_GROUPS)
             nc.sync.dma_start(out=noise_sb[:, some, :], in_=noise_rows[:, some, :])
             nc.sync.dma_start(out=lr_sb[:, some, :], in_=lr_rows[:, some, :])
-            if g0 == 0:
+            if g0 == LOAD_GROUPS:
                 load_weight(nc, wc_words, wc_plane, W_cls_words, W_cls_scales)
 
         ident = keep.tile([P, P], F32)
         make_identity(nc, ident[:])
+        ones = keep.tile([P, P], BF16)
+        nc.vector.memset(ones[:], 1.0)
         one = keep.tile([P, 1], F32)
         nc.vector.memset(one[:], 1.0)
         warm = keep.tile([P, 1], F32)
         nc.scalar.activation(out=warm[:], in_=one[:], func=ACT.Exp)
+
+        noiseT_sb = keep.tile([P, GROUPS, HALVES, ROWS_PER_Q, P], F32)
+        lr_grouped = keep.tile([P, GROUPS, GROUP_ROWS, PACK], BF16)
 
         def flip_words(dst, rows_bf16, first_word):
             words = rows_bf16.bitcast(F32)
@@ -95,7 +101,7 @@ def tile_hetxlhead_pa_kernel(
                 )
 
         def interleave(grouped, bank_words):
-            dst = grouped[:].rearrange("p r t -> p (r t)").bitcast(F32).rearrange("p (r u) -> p r u", u=HALVES)
+            dst = grouped.rearrange("p r t -> p (r t)").bitcast(F32).rearrange("p (r u) -> p r u", u=HALVES)
             return dst, bank_words.rearrange("p u r -> p r u")
 
         def flip_group(g):
@@ -106,13 +112,19 @@ def tile_hetxlhead_pa_kernel(
                     flip_words([bank[:, u, sl, :] for u in range(HALVES)], rows[:, g, :], sl * (D // 2))
             return noiseT, lrT
 
-        def scale_noise(g, noiseT, lrT):
-            lr_grouped = work.tile([P, GROUP_ROWS, PACK], BF16)
-            dst, src = interleave(lr_grouped, lrT[:].rearrange("p u sl q -> p u (sl q)"))
-            nc.scalar.copy(out=dst, in_=src)
+        def copy_group(g, noiseT, lrT):
+            dst, src = interleave(lr_grouped[:, g, :, :], lrT[:].rearrange("p u sl q -> p u (sl q)"))
+            if g < VECTOR_COPIES:
+                nc.vector.tensor_copy(out=noiseT_sb[:, g, :, :, :], in_=noiseT[:])
+                nc.vector.tensor_copy(out=dst, in_=src)
+            else:
+                nc.scalar.copy(out=noiseT_sb[:, g, :, :, :], in_=noiseT[:])
+                nc.scalar.copy(out=dst, in_=src)
+
+        def scale_noise(g):
             scaled = work.tile([P, PACK, ROWS_PER_Q, P], F32)
             pairs = (
-                noiseT[:]
+                noiseT_sb[:, g, :, :, :]
                 .rearrange("p u sl q -> p (u sl q)")
                 .bitcast(BF16)
                 .rearrange("p (u sl q e) -> p u sl q e", u=HALVES, sl=ROWS_PER_Q, e=2)
@@ -128,12 +140,12 @@ def tile_hetxlhead_pa_kernel(
                         scale=stdT[:, t, b : b + 1],
                         bias=fT[:, t, b : b + 1],
                     )
-            return scaled, lr_grouped
+            return scaled
 
-        def add_lr(scaled, lr_grouped):
+        def add_lr(g, scaled):
             pre = work.tile([P, GROUP_ROWS, PACK], BF16, align_bytes=64)
             nc.gpsimd.tensor_tensor(
-                out=pre[:], in0=scaled[:].rearrange("p t sl q -> p (sl q) t"), in1=lr_grouped[:], op=ALU.add
+                out=pre[:], in0=scaled[:].rearrange("p t sl q -> p (sl q) t"), in1=lr_grouped[:, g, :, :], op=ALU.add
             )
             return pre
 
@@ -165,22 +177,24 @@ def tile_hetxlhead_pa_kernel(
             return parts
 
         def finish(g, parts):
-            logits = store.tile([P, ROWS_PER_Q, C], F32)
-            for sl, its_classes, acc in parts:
-                nc.vector.scalar_tensor_tensor(
-                    out=logits[:, sl, its_classes],
-                    in0=acc[:],
-                    scalar=INV_TEMPERATURE,
-                    in1=bias_scaled[:, its_classes],
-                    op0=ALU.mult,
-                    op1=ALU.add,
-                )
-            nc.sync.dma_start(out=out_rows[:, g, :], in_=logits[:].rearrange("q sl c -> q (sl c)"))
+            for sl in range(ROWS_PER_Q):
+                logits = store.tile([P, C], F32)
+                for its_sl, its_classes, acc in parts:
+                    if its_sl == sl:
+                        nc.vector.scalar_tensor_tensor(
+                            out=logits[:, its_classes],
+                            in0=acc[:],
+                            scalar=INV_TEMPERATURE,
+                            in1=bias_scaled[:, its_classes],
+                            op0=ALU.mult,
+                            op1=ALU.add,
+                        )
+                nc.sync.dma_start(out=out_rows[:, g, sl, :], in_=logits[:])
 
         fT_ps = sums.tile([P, HALVES, B], F32, tag="acc")
         flip_words([fT_ps[:, u, :] for u in range(HALVES)], f_sb[:], 0)
         f_grouped = keep.tile([P, B, PACK], BF16, align_bytes=64)
-        dst, src = interleave(f_grouped, fT_ps[:])
+        dst, src = interleave(f_grouped[:], fT_ps[:])
         nc.vector.tensor_copy(out=dst, in_=src)
         f_codes = keep.tile([P, B], U32, align_bytes=64)
         f_scales = keep.tile([P, B], U8, align_bytes=64)
@@ -189,6 +203,18 @@ def tile_hetxlhead_pa_kernel(
         )
         fT = keep.tile([P, PACK, B], F32)
         nc.scalar.copy(out=fT[:], in_=f_grouped[:].rearrange("p b t -> p t b"))
+
+        bdiag_ps = sums.tile([P, D], F32, tag="acc")
+        nc.tensor.matmul(out=bdiag_ps[:], lhsT=ones[:], rhs=bias_rows[:, 0:D], start=True, stop=True)
+        bdiag_all = keep.tile([P, D], F32)
+        nc.vector.tensor_copy(out=bdiag_all[:], in_=bdiag_ps[:])
+        bias_scaled = keep.tile([P, C], F32)
+        for n0 in range(0, C, N_TILE):
+            bcls_ps = sums.tile([P, N_TILE], F32, tag="acc")
+            nc.tensor.matmul(
+                out=bcls_ps[:], lhsT=ones[:], rhs=bias_rows[:, D + n0 : D + n0 + N_TILE], start=True, stop=True
+            )
+            nc.scalar.mul(out=bias_scaled[:, n0 : n0 + N_TILE], in_=bcls_ps[:], mul=INV_TEMPERATURE)
 
         z_ps = sums.tile([P, D], F32, tag="acc")
         nc.tensor.matmul_mx(
@@ -200,7 +226,6 @@ def tile_hetxlhead_pa_kernel(
             start=True,
             stop=True,
         )
-        banks = {0: flip_group(0), 1: flip_group(1)}
         z = keep.tile([P, D], F32)
         nc.vector.tensor_tensor(out=z[:], in0=z_ps[:], in1=bdiag_all[:], op=ALU.add)
         tail = keep.tile([P, D], F32)
@@ -209,6 +234,9 @@ def tile_hetxlhead_pa_kernel(
         nc.scalar.activation(out=tail[:], in_=tail[:], func=ACT.Ln, bias=one[:])
         ramp = keep.tile([P, D], F32)
         nc.vector.tensor_scalar(out=ramp[:], in0=z[:], scalar1=0.0, scalar2=MIN_SCALE, op0=ALU.max, op1=ALU.add)
+        for g in range(2):
+            noiseT, lrT = flip_group(g)
+            copy_group(g, noiseT, lrT)
         std_sorted = keep.tile([P, PACK, P], F32)
         nc.vector.tensor_tensor(
             out=std_sorted[:],
@@ -221,23 +249,24 @@ def tile_hetxlhead_pa_kernel(
             nc.tensor.transpose(out=stdT_ps[:, t, :], in_=std_sorted[:, t, :], identity=ident[:])
         stdT = keep.tile([P, PACK, B], F32)
         nc.vector.tensor_copy(out=stdT[:], in_=stdT_ps[:])
-        bias_scaled = keep.tile([P, C], F32)
-        nc.vector.tensor_scalar(
-            out=bias_scaled[:], in0=bcls_all[:], scalar1=INV_TEMPERATURE, scalar2=None, op0=ALU.mult
-        )
+        for g in range(2, VECTOR_COPIES):
+            noiseT, lrT = flip_group(g)
+            copy_group(g, noiseT, lrT)
 
         pres = {}
         accs = {}
         for g in range(GROUPS + 2):
+            ahead = g + VECTOR_COPIES
+            if ahead < GROUPS:
+                noiseT, lrT = flip_group(ahead)
             if g < GROUPS:
-                noiseT, lrT = banks[g]
-                scaled, lr_grouped = scale_noise(g, noiseT, lrT)
-                pres[g] = add_lr(scaled, lr_grouped)
+                scaled = scale_noise(g)
+                pres[g] = add_lr(g, scaled)
+            if ahead < GROUPS:
+                copy_group(ahead, noiseT, lrT)
             if 1 <= g <= GROUPS:
                 codes, scales = quantise(pres[g - 1])
             if g >= 2:
                 finish(g - 2, accs[g - 2])
             if 1 <= g <= GROUPS:
                 accs[g - 1] = multiply(codes, scales)
-            if g + 2 < GROUPS:
-                banks[g + 2] = flip_group(g + 2)

@@ -144,7 +144,8 @@ def tile_hetxlhead_pa_kernel(
 
         def add_lr(g, scaled):
             pre = work.tile([P, GROUP_ROWS, PACK], BF16, align_bytes=64)
-            nc.gpsimd.tensor_tensor(
+            engine = nc.gpsimd if g % 2 == 0 else nc.vector
+            engine.tensor_tensor(
                 out=pre[:], in0=scaled[:].rearrange("p t sl q -> p (sl q) t"), in1=lr_grouped[:, g, :, :], op=ALU.add
             )
             return pre
@@ -261,7 +262,6 @@ def tile_hetxlhead_pa_kernel(
                 noiseT, lrT = flip_group(ahead)
             if g < GROUPS:
                 scaled = scale_noise(g)
-                pres[g] = add_lr(g, scaled)
             if ahead < GROUPS:
                 copy_group(ahead, noiseT, lrT)
             if 1 <= g <= GROUPS:
@@ -270,3 +270,5 @@ def tile_hetxlhead_pa_kernel(
                 finish(g - 2, accs[g - 2])
             if 1 <= g <= GROUPS:
                 accs[g - 1] = multiply(codes, scales)
+            if g < GROUPS:
+                pres[g] = add_lr(g, scaled)

@@ -132,7 +132,7 @@ def tile_hetxlhead_pa_kernel(
             for i in range(B_PER_GROUP):
                 b = g * B_PER_GROUP + i
                 its_q = slice(i * Q_PER_B, (i + 1) * Q_PER_B)
-                for t in range(PACK):
+                for t in range(PACK - 1):
                     nc.scalar.activation(
                         out=scaled[:, t, :, its_q],
                         in_=pairs[:, t // 2, :, its_q, t % 2],
@@ -140,12 +140,20 @@ def tile_hetxlhead_pa_kernel(
                         scale=stdT[:, t, b : b + 1],
                         bias=fT[:, t, b : b + 1],
                     )
+                t = PACK - 1
+                nc.vector.tensor_scalar(
+                    out=scaled[:, t, :, its_q],
+                    in0=pairs[:, t // 2, :, its_q, t % 2],
+                    scalar1=stdT[:, t, b : b + 1],
+                    scalar2=fT[:, t, b : b + 1],
+                    op0=ALU.mult,
+                    op1=ALU.add,
+                )
             return scaled
 
         def add_lr(g, scaled):
             pre = work.tile([P, GROUP_ROWS, PACK], BF16, align_bytes=64)
-            engine = nc.gpsimd if g % 2 == 0 else nc.vector
-            engine.tensor_tensor(
+            nc.gpsimd.tensor_tensor(
                 out=pre[:], in0=scaled[:].rearrange("p t sl q -> p (sl q) t"), in1=lr_grouped[:, g, :, :], op=ALU.add
             )
             return pre
@@ -262,6 +270,7 @@ def tile_hetxlhead_pa_kernel(
                 noiseT, lrT = flip_group(ahead)
             if g < GROUPS:
                 scaled = scale_noise(g)
+                pres[g] = add_lr(g, scaled)
             if ahead < GROUPS:
                 copy_group(ahead, noiseT, lrT)
             if 1 <= g <= GROUPS:
@@ -270,5 +279,3 @@ def tile_hetxlhead_pa_kernel(
                 finish(g - 2, accs[g - 2])
             if 1 <= g <= GROUPS:
                 accs[g - 1] = multiply(codes, scales)
-            if g < GROUPS:
-                pres[g] = add_lr(g, scaled)

@@ -19,14 +19,13 @@ INV_TEMPERATURE = 1.0 / 1.5
 P = 128
 PACK = 4
 HALVES = 2
-ROWS_PER_Q = 2
-GROUP_ROWS = P * ROWS_PER_Q
-GROUPS = B * S // GROUP_ROWS
-B_PER_GROUP = GROUP_ROWS // S
-Q_PER_B = P // B_PER_GROUP
 N_TILE = 512
-LOAD_GROUPS = 2
-VECTOR_COPIES = 6
+PAIR = 2
+ROUNDS = S // PAIR
+LOAD_TILES = 4
+SUM_ROUNDS = 3
+VECTOR_ROUNDS = 2
+SLOTS = 3
 
 FLOPS = 2 * B * D * D + 2 * B * S * D * C
 
@@ -46,38 +45,43 @@ def tile_hetxlhead_pa_kernel(
     tc, features, W_diag_words, W_diag_scales, b_diag, W_cls_words, W_cls_scales, b_cls, noise_diag, lr_samples, out
 ):
     nc = tc.nc
-    noise_rows = noise_diag.flatten_outer_dims().rearrange("(g q sl) d -> q g (sl d)", q=P, sl=ROWS_PER_Q)
-    lr_rows = lr_samples.flatten_outer_dims().rearrange("(g q sl) d -> q g (sl d)", q=P, sl=ROWS_PER_Q)
-    out_rows = out.flatten_outer_dims().rearrange("(g q sl) c -> q g sl c", q=P, sl=ROWS_PER_Q)
 
     with ExitStack() as stack:
         keep = stack.enter_context(tc.tile_pool(name="keep", bufs=1))
+        shared = stack.enter_context(tc.tile_pool(name="shared", bufs=1))
         work = stack.enter_context(tc.tile_pool(name="work", bufs=3))
         store = stack.enter_context(tc.tile_pool(name="store", bufs=6))
-        flipped = stack.enter_context(tc.psum_pool(name="flipped", bufs=2))
+        flipped = stack.enter_context(tc.psum_pool(name="flipped", bufs=4))
         sums = stack.enter_context(tc.psum_pool(name="sums", bufs=4))
         stack.enter_context(tc.manual_schedule())
 
         f_sb = keep.tile([P, D], BF16)
         nc.sync.dma_start(out=f_sb[:], in_=features)
+        wd_words = keep.tile([P, D], U32, align_bytes=64)
+        wd_plane = keep.tile([P, D], U8, align_bytes=64)
+        load_weight(nc, wd_words, wd_plane, W_diag_words, W_diag_scales)
         bias_rows = keep.tile([P, D + C], BF16)
         nc.vector.memset(bias_rows[:].bitcast(I32), 0)
         nc.sync.dma_start(out=bias_rows[0:1, 0:D], in_=b_diag.unsqueeze(0))
         nc.sync.dma_start(out=bias_rows[0:1, D : D + C], in_=b_cls.unsqueeze(0))
-        wd_words = keep.tile([P, D], U32, align_bytes=64)
-        wd_plane = keep.tile([P, D], U8, align_bytes=64)
-        load_weight(nc, wd_words, wd_plane, W_diag_words, W_diag_scales)
 
-        noise_sb = keep.tile([P, GROUPS, ROWS_PER_Q * D], BF16)
-        lr_sb = keep.tile([P, GROUPS, ROWS_PER_Q * D], BF16)
+        noise_sb = keep.tile([P, S, D], BF16)
+        lr_sb = keep.tile([P, S, D], BF16)
         wc_words = keep.tile([P, C], U32, align_bytes=64)
         wc_plane = keep.tile([P, C], U8, align_bytes=64)
-        for g0 in range(0, GROUPS, LOAD_GROUPS):
-            some = slice(g0, g0 + LOAD_GROUPS)
-            nc.sync.dma_start(out=noise_sb[:, some, :], in_=noise_rows[:, some, :])
-            nc.sync.dma_start(out=lr_sb[:, some, :], in_=lr_rows[:, some, :])
-            if g0 == LOAD_GROUPS:
-                load_weight(nc, wc_words, wc_plane, W_cls_words, W_cls_scales)
+
+        def load_tiles(dst, src, first):
+            some = slice(first, first + LOAD_TILES)
+            nc.sync.dma_start(out=dst[:, some, :], in_=src[:, some, :])
+
+        load_tiles(lr_sb, lr_samples, 0)
+        load_tiles(lr_sb, lr_samples, LOAD_TILES)
+        load_tiles(noise_sb, noise_diag, 0)
+        load_weight(nc, wc_words, wc_plane, W_cls_words, W_cls_scales)
+        load_tiles(noise_sb, noise_diag, LOAD_TILES)
+        for first in range(2 * LOAD_TILES, S, LOAD_TILES):
+            load_tiles(lr_sb, lr_samples, first)
+            load_tiles(noise_sb, noise_diag, first)
 
         ident = keep.tile([P, P], F32)
         make_identity(nc, ident[:])
@@ -88,142 +92,35 @@ def tile_hetxlhead_pa_kernel(
         warm = keep.tile([P, 1], F32)
         nc.scalar.activation(out=warm[:], in_=one[:], func=ACT.Exp)
 
-        noiseT_sb = keep.tile([P, GROUPS, HALVES, ROWS_PER_Q, P], F32)
-        lr_grouped = keep.tile([P, GROUPS, GROUP_ROWS, PACK], BF16)
+        def by_t(rows):
+            if rows.ndim == 2:
+                return rows.rearrange("b (p t) -> b t p", t=PACK)
+            return rows.rearrange("b s (p t) -> b s t p", t=PACK)
 
-        def flip_words(dst, rows_bf16, first_word):
-            words = rows_bf16.bitcast(F32)
-            for u in range(HALVES):
-                nc.tensor.transpose(
-                    out=dst[u],
-                    in_=words[:, first_word + u : first_word + D // 2 : HALVES],
-                    identity=ident[:],
-                )
-
-        def interleave(grouped, bank_words):
-            dst = grouped.rearrange("p r t -> p (r t)").bitcast(F32).rearrange("p (r u) -> p r u", u=HALVES)
-            return dst, bank_words.rearrange("p u r -> p r u")
-
-        def flip_group(g):
-            noiseT = flipped.tile([P, HALVES, ROWS_PER_Q, P], F32, tag="noiseT")
-            lrT = flipped.tile([P, HALVES, ROWS_PER_Q, P], F32, tag="lrT")
-            for bank, rows in ((noiseT, noise_sb), (lrT, lr_sb)):
-                for sl in range(ROWS_PER_Q):
-                    flip_words([bank[:, u, sl, :] for u in range(HALVES)], rows[:, g, :], sl * (D // 2))
-            return noiseT, lrT
-
-        def copy_group(g, noiseT, lrT):
-            dst, src = interleave(lr_grouped[:, g, :, :], lrT[:].rearrange("p u sl q -> p u (sl q)"))
-            if g < VECTOR_COPIES:
-                nc.vector.tensor_copy(out=noiseT_sb[:, g, :, :, :], in_=noiseT[:])
-                nc.vector.tensor_copy(out=dst, in_=src)
-            else:
-                nc.scalar.copy(out=noiseT_sb[:, g, :, :, :], in_=noiseT[:])
-                nc.scalar.copy(out=dst, in_=src)
-
-        def scale_noise(g):
-            scaled = work.tile([P, PACK, ROWS_PER_Q, P], F32)
-            pairs = (
-                noiseT_sb[:, g, :, :, :]
-                .rearrange("p u sl q -> p (u sl q)")
-                .bitcast(BF16)
-                .rearrange("p (u sl q e) -> p u sl q e", u=HALVES, sl=ROWS_PER_Q, e=2)
-            )
-            for i in range(B_PER_GROUP):
-                b = g * B_PER_GROUP + i
-                its_q = slice(i * Q_PER_B, (i + 1) * Q_PER_B)
-                for t in range(PACK - 1):
-                    nc.scalar.activation(
-                        out=scaled[:, t, :, its_q],
-                        in_=pairs[:, t // 2, :, its_q, t % 2],
-                        func=ACT.Identity,
-                        scale=stdT[:, t, b : b + 1],
-                        bias=fT[:, t, b : b + 1],
-                    )
-                t = PACK - 1
-                nc.vector.tensor_scalar(
-                    out=scaled[:, t, :, its_q],
-                    in0=pairs[:, t // 2, :, its_q, t % 2],
-                    scalar1=stdT[:, t, b : b + 1],
-                    scalar2=fT[:, t, b : b + 1],
-                    op0=ALU.mult,
-                    op1=ALU.add,
-                )
-            return scaled
-
-        def add_lr(g, scaled):
-            pre = work.tile([P, GROUP_ROWS, PACK], BF16, align_bytes=64)
-            nc.gpsimd.tensor_tensor(
-                out=pre[:], in0=scaled[:].rearrange("p t sl q -> p (sl q) t"), in1=lr_grouped[:, g, :, :], op=ALU.add
-            )
-            return pre
-
-        def quantise(pre):
-            codes = work.tile([P, GROUP_ROWS], U32, align_bytes=64)
-            scales = work.tile([P, GROUP_ROWS], U8, align_bytes=64)
-            nc.vector.quantize_mx(
-                out=codes[:].bitcast(FP8X4), scales=scales[:], in_=pre[:].rearrange("p r t -> p (r t)")
-            )
-            return codes, scales
-
-        def multiply(codes, scales):
-            parts = []
-            for sl in range(ROWS_PER_Q):
-                its_rows = slice(sl * P, (sl + 1) * P)
-                for n0 in range(0, C, N_TILE):
-                    its_classes = slice(n0, n0 + N_TILE)
-                    acc = sums.tile([P, N_TILE], F32, tag="acc")
-                    nc.tensor.matmul_mx(
-                        out=acc[:],
-                        lhsT=codes[:, its_rows].bitcast(FP8X4),
-                        lhsT_scale=scales[:, its_rows],
-                        rhs=wc_words[:, its_classes].bitcast(FP8X4),
-                        rhs_scale=wc_plane[:, its_classes],
-                        start=True,
-                        stop=True,
-                    )
-                    parts.append((sl, its_classes, acc))
-            return parts
-
-        def finish(g, parts):
-            for sl in range(ROWS_PER_Q):
-                logits = store.tile([P, C], F32)
-                for its_sl, its_classes, acc in parts:
-                    if its_sl == sl:
-                        nc.vector.scalar_tensor_tensor(
-                            out=logits[:, its_classes],
-                            in0=acc[:],
-                            scalar=INV_TEMPERATURE,
-                            in1=bias_scaled[:, its_classes],
-                            op0=ALU.mult,
-                            op1=ALU.add,
-                        )
-                nc.sync.dma_start(out=out_rows[:, g, sl, :], in_=logits[:])
+        def for_pair(row):
+            return row.unsqueeze(1).to_broadcast([P, PAIR, PACK, P])
 
         fT_ps = sums.tile([P, HALVES, B], F32, tag="acc")
-        flip_words([fT_ps[:, u, :] for u in range(HALVES)], f_sb[:], 0)
+        f_words = f_sb[:].bitcast(F32)
+        for u in range(HALVES):
+            nc.tensor.transpose(out=fT_ps[:, u, :], in_=f_words[:, u : D // 2 : HALVES], identity=ident[:])
         f_grouped = keep.tile([P, B, PACK], BF16, align_bytes=64)
-        dst, src = interleave(f_grouped[:], fT_ps[:])
-        nc.vector.tensor_copy(out=dst, in_=src)
+        nc.vector.tensor_copy(
+            out=f_grouped[:].rearrange("p b t -> p (b t)").bitcast(F32).rearrange("p (b u) -> p b u", u=HALVES),
+            in_=fT_ps[:].rearrange("p u b -> p b u"),
+        )
         f_codes = keep.tile([P, B], U32, align_bytes=64)
         f_scales = keep.tile([P, B], U8, align_bytes=64)
         nc.vector.quantize_mx(
             out=f_codes[:].bitcast(FP8X4), scales=f_scales[:], in_=f_grouped[:].rearrange("p b t -> p (b t)")
         )
-        fT = keep.tile([P, PACK, B], F32)
-        nc.scalar.copy(out=fT[:], in_=f_grouped[:].rearrange("p b t -> p t b"))
+        f_term = keep.tile([P, PACK, P], F32)
+        nc.scalar.copy(out=f_term[:], in_=by_t(f_sb[:]))
 
         bdiag_ps = sums.tile([P, D], F32, tag="acc")
         nc.tensor.matmul(out=bdiag_ps[:], lhsT=ones[:], rhs=bias_rows[:, 0:D], start=True, stop=True)
         bdiag_all = keep.tile([P, D], F32)
-        nc.vector.tensor_copy(out=bdiag_all[:], in_=bdiag_ps[:])
-        bias_scaled = keep.tile([P, C], F32)
-        for n0 in range(0, C, N_TILE):
-            bcls_ps = sums.tile([P, N_TILE], F32, tag="acc")
-            nc.tensor.matmul(
-                out=bcls_ps[:], lhsT=ones[:], rhs=bias_rows[:, D + n0 : D + n0 + N_TILE], start=True, stop=True
-            )
-            nc.scalar.mul(out=bias_scaled[:, n0 : n0 + N_TILE], in_=bcls_ps[:], mul=INV_TEMPERATURE)
+        nc.scalar.copy(out=bdiag_all[:], in_=bdiag_ps[:])
 
         z_ps = sums.tile([P, D], F32, tag="acc")
         nc.tensor.matmul_mx(
@@ -243,39 +140,129 @@ def tile_hetxlhead_pa_kernel(
         nc.scalar.activation(out=tail[:], in_=tail[:], func=ACT.Ln, bias=one[:])
         ramp = keep.tile([P, D], F32)
         nc.vector.tensor_scalar(out=ramp[:], in0=z[:], scalar1=0.0, scalar2=MIN_SCALE, op0=ALU.max, op1=ALU.add)
-        for g in range(2):
-            noiseT, lrT = flip_group(g)
-            copy_group(g, noiseT, lrT)
-        std_sorted = keep.tile([P, PACK, P], F32)
-        nc.vector.tensor_tensor(
-            out=std_sorted[:],
-            in0=ramp[:].rearrange("b (p t) -> b t p", t=PACK),
-            in1=tail[:].rearrange("b (p t) -> b t p", t=PACK),
-            op=ALU.add,
-        )
-        stdT_ps = sums.tile([P, PACK, B], F32, tag="acc")
-        for t in range(PACK):
-            nc.tensor.transpose(out=stdT_ps[:, t, :], in_=std_sorted[:, t, :], identity=ident[:])
-        stdT = keep.tile([P, PACK, B], F32)
-        nc.vector.tensor_copy(out=stdT[:], in_=stdT_ps[:])
-        for g in range(2, VECTOR_COPIES):
-            noiseT, lrT = flip_group(g)
-            copy_group(g, noiseT, lrT)
 
+        bias_scaled = keep.tile([P, C], F32)
+        for n0 in range(0, C, N_TILE):
+            bcls_ps = sums.tile([P, N_TILE], F32, tag="acc")
+            nc.tensor.matmul(
+                out=bcls_ps[:], lhsT=ones[:], rhs=bias_rows[:, D + n0 : D + n0 + N_TILE], start=True, stop=True
+            )
+            nc.scalar.mul(out=bias_scaled[:, n0 : n0 + N_TILE], in_=bcls_ps[:], mul=INV_TEMPERATURE)
+
+        lr_term = keep.tile([P, S, PACK, P], F32)
+
+        def its_tiles(r):
+            return slice(r * PAIR, (r + 1) * PAIR)
+
+        def sum_lr(r):
+            nc.vector.tensor_tensor(
+                out=lr_term[:, its_tiles(r), :, :], in0=by_t(lr_sb[:, its_tiles(r), :]), in1=for_pair(f_term[:]), op=ALU.add
+            )
+
+        def widen_lr(r):
+            nc.scalar.copy(out=lr_term[:, its_tiles(r), :, :], in_=by_t(lr_sb[:, its_tiles(r), :]))
+
+        def scale_noise(r):
+            product = shared.tile([P, PAIR, PACK, P], F32, tag="slot%d" % (r % SLOTS), align_bytes=64)
+            if r < VECTOR_ROUNDS:
+                for j in range(PAIR):
+                    nc.vector.tensor_tensor(
+                        out=product[:, j, :, :], in0=by_t(noise_sb[:, r * PAIR + j, :]), in1=std_term[:], op=ALU.mult
+                    )
+            else:
+                nc.gpsimd.tensor_tensor(
+                    out=product[:], in0=by_t(noise_sb[:, its_tiles(r), :]), in1=for_pair(std_term[:]), op=ALU.mult
+                )
+            return product
+
+        def flip(r, product):
+            banks = []
+            for j in range(PAIR):
+                bank = flipped.tile([P, PACK, B], F32, tag="preT")
+                for t in range(PACK):
+                    terms = [lr_term[:, r * PAIR + j, t, :]]
+                    if r >= SUM_ROUNDS:
+                        terms.append(f_term[:, t, :])
+                    terms.append(product[:, j, t, :])
+                    for i, term in enumerate(terms):
+                        nc.tensor.matmul(
+                            out=bank[:, t, :],
+                            lhsT=term,
+                            rhs=ident[:],
+                            is_transpose=True,
+                            start=(i == 0),
+                            stop=(i == len(terms) - 1),
+                        )
+                banks.append(bank)
+            return banks
+
+        def round_off(r, banks):
+            pre = shared.tile([P, PAIR, B, PACK], BF16, tag="slot%d" % ((r + SLOTS - 1) % SLOTS), align_bytes=64)
+            for j in range(PAIR):
+                nc.scalar.copy(out=pre[:, j, :, :], in_=banks[j][:].rearrange("p t b -> p b t"))
+            return pre
+
+        def quantise(pre):
+            codes = work.tile([P, PAIR * B], U32, align_bytes=64)
+            scales = work.tile([P, PAIR * B], U8, align_bytes=64)
+            nc.vector.quantize_mx(
+                out=codes[:].bitcast(FP8X4), scales=scales[:], in_=pre[:].rearrange("p j b t -> p (j b t)")
+            )
+            return codes, scales
+
+        def multiply(codes, scales):
+            parts = []
+            for j in range(PAIR):
+                its_rows = slice(j * B, (j + 1) * B)
+                for n0 in range(0, C, N_TILE):
+                    its_classes = slice(n0, n0 + N_TILE)
+                    acc = sums.tile([P, N_TILE], F32, tag="acc")
+                    nc.tensor.matmul_mx(
+                        out=acc[:],
+                        lhsT=codes[:, its_rows].bitcast(FP8X4),
+                        lhsT_scale=scales[:, its_rows],
+                        rhs=wc_words[:, its_classes].bitcast(FP8X4),
+                        rhs_scale=wc_plane[:, its_classes],
+                        start=True,
+                        stop=True,
+                    )
+                    parts.append((j, its_classes, acc))
+            return parts
+
+        def finish(r, parts):
+            for j in range(PAIR):
+                logits = store.tile([P, C], F32)
+                for its_j, its_classes, acc in parts:
+                    if its_j == j:
+                        nc.vector.scalar_tensor_tensor(
+                            out=logits[:, its_classes],
+                            in0=acc[:],
+                            scalar=INV_TEMPERATURE,
+                            in1=bias_scaled[:, its_classes],
+                            op0=ALU.mult,
+                            op1=ALU.add,
+                        )
+                nc.sync.dma_start(out=out[:, r * PAIR + j, :], in_=logits[:])
+
+        for r in range(SUM_ROUNDS):
+            sum_lr(r)
+        std_term = keep.tile([P, PACK, P], F32)
+        nc.vector.tensor_tensor(out=std_term[:], in0=by_t(ramp[:]), in1=by_t(tail[:]), op=ALU.add)
+
+        products = {}
         pres = {}
         accs = {}
-        for g in range(GROUPS + 2):
-            ahead = g + VECTOR_COPIES
-            if ahead < GROUPS:
-                noiseT, lrT = flip_group(ahead)
-            if g < GROUPS:
-                scaled = scale_noise(g)
-                pres[g] = add_lr(g, scaled)
-            if ahead < GROUPS:
-                copy_group(ahead, noiseT, lrT)
-            if 1 <= g <= GROUPS:
-                codes, scales = quantise(pres[g - 1])
-            if g >= 2:
-                finish(g - 2, accs[g - 2])
-            if 1 <= g <= GROUPS:
-                accs[g - 1] = multiply(codes, scales)
+        for n in range(-2, ROUNDS + 1):
+            if 0 <= n < ROUNDS:
+                codes, scales = quantise(pres[n])
+            if 0 <= n + 2 < ROUNDS:
+                products[n + 2] = scale_noise(n + 2)
+            if SUM_ROUNDS <= n + 4 < ROUNDS:
+                widen_lr(n + 4)
+            if 0 <= n + 1 < ROUNDS:
+                banks = flip(n + 1, products[n + 1])
+                pres[n + 1] = round_off(n + 1, banks)
+            if 0 <= n < ROUNDS:
+                accs[n] = multiply(codes, scales)
+            if n >= 1:
+                finish(n - 1, accs[n - 1])

@@ -26,6 +26,7 @@ LOAD_TILES = 4
 SUM_ROUNDS = 3
 VECTOR_ROUNDS = 2
 SLOTS = 3
+PLAIN_ROUNDS = 11
 
 FLOPS = 2 * B * D * D + 2 * B * S * D * C
 
@@ -51,19 +52,18 @@ def tile_hetxlhead_pa_kernel(
         shared = stack.enter_context(tc.tile_pool(name="shared", bufs=1))
         work = stack.enter_context(tc.tile_pool(name="work", bufs=3))
         store = stack.enter_context(tc.tile_pool(name="store", bufs=6))
-        flipped = stack.enter_context(tc.psum_pool(name="flipped", bufs=4))
-        sums = stack.enter_context(tc.psum_pool(name="sums", bufs=4))
+        banks_pool = stack.enter_context(tc.psum_pool(name="banks", bufs=8))
         stack.enter_context(tc.manual_schedule())
 
         f_sb = keep.tile([P, D], BF16)
         nc.sync.dma_start(out=f_sb[:], in_=features)
-        wd_words = keep.tile([P, D], U32, align_bytes=64)
-        wd_plane = keep.tile([P, D], U8, align_bytes=64)
-        load_weight(nc, wd_words, wd_plane, W_diag_words, W_diag_scales)
         bias_rows = keep.tile([P, D + C], BF16)
         nc.vector.memset(bias_rows[:].bitcast(I32), 0)
         nc.sync.dma_start(out=bias_rows[0:1, 0:D], in_=b_diag.unsqueeze(0))
         nc.sync.dma_start(out=bias_rows[0:1, D : D + C], in_=b_cls.unsqueeze(0))
+        wd_words = keep.tile([P, D], U32, align_bytes=64)
+        wd_plane = keep.tile([P, D], U8, align_bytes=64)
+        load_weight(nc, wd_words, wd_plane, W_diag_words, W_diag_scales)
 
         noise_sb = keep.tile([P, S, D], BF16)
         lr_sb = keep.tile([P, S, D], BF16)
@@ -85,6 +85,8 @@ def tile_hetxlhead_pa_kernel(
 
         ident = keep.tile([P, P], F32)
         make_identity(nc, ident[:])
+        ident_half = keep.tile([P, P], BF16)
+        make_identity(nc, ident_half[:])
         ones = keep.tile([P, P], BF16)
         nc.vector.memset(ones[:], 1.0)
         one = keep.tile([P, 1], F32)
@@ -100,7 +102,7 @@ def tile_hetxlhead_pa_kernel(
         def for_pair(row):
             return row.unsqueeze(1).to_broadcast([P, PAIR, PACK, P])
 
-        fT_ps = sums.tile([P, HALVES, B], F32, tag="acc")
+        fT_ps = banks_pool.tile([P, HALVES, B], F32, tag="bank")
         f_words = f_sb[:].bitcast(F32)
         for u in range(HALVES):
             nc.tensor.transpose(out=fT_ps[:, u, :], in_=f_words[:, u : D // 2 : HALVES], identity=ident[:])
@@ -116,13 +118,15 @@ def tile_hetxlhead_pa_kernel(
         )
         f_term = keep.tile([P, PACK, P], F32)
         nc.scalar.copy(out=f_term[:], in_=by_t(f_sb[:]))
+        f_half = keep.tile([P, PACK, P], BF16)
+        nc.scalar.copy(out=f_half[:], in_=by_t(f_sb[:]))
 
-        bdiag_ps = sums.tile([P, D], F32, tag="acc")
+        bdiag_ps = banks_pool.tile([P, D], F32, tag="bank")
         nc.tensor.matmul(out=bdiag_ps[:], lhsT=ones[:], rhs=bias_rows[:, 0:D], start=True, stop=True)
         bdiag_all = keep.tile([P, D], F32)
         nc.scalar.copy(out=bdiag_all[:], in_=bdiag_ps[:])
 
-        z_ps = sums.tile([P, D], F32, tag="acc")
+        z_ps = banks_pool.tile([P, D], F32, tag="bank")
         nc.tensor.matmul_mx(
             out=z_ps[:],
             lhsT=f_codes[:].bitcast(FP8X4),
@@ -143,7 +147,7 @@ def tile_hetxlhead_pa_kernel(
 
         bias_scaled = keep.tile([P, C], F32)
         for n0 in range(0, C, N_TILE):
-            bcls_ps = sums.tile([P, N_TILE], F32, tag="acc")
+            bcls_ps = banks_pool.tile([P, N_TILE], F32, tag="bank")
             nc.tensor.matmul(
                 out=bcls_ps[:], lhsT=ones[:], rhs=bias_rows[:, D + n0 : D + n0 + N_TILE], start=True, stop=True
             )
@@ -175,26 +179,40 @@ def tile_hetxlhead_pa_kernel(
                 )
             return product
 
-        def flip(r, product):
+        def flip_terms(bank, terms, opens, closes):
+            for i, term in enumerate(terms):
+                for t in range(PACK):
+                    nc.tensor.matmul(
+                        out=bank[:, t, :],
+                        lhsT=term[:, t, :],
+                        rhs=ident[:],
+                        is_transpose=True,
+                        start=(opens and i == 0 and t == 0),
+                        stop=(closes and i == len(terms) - 1 and t == PACK - 1),
+                    )
+
+        def open_banks(r):
             banks = []
             for j in range(PAIR):
-                bank = flipped.tile([P, PACK, B], F32, tag="preT")
-                for t in range(PACK):
-                    terms = [lr_term[:, r * PAIR + j, t, :]]
-                    if r >= SUM_ROUNDS:
-                        terms.append(f_term[:, t, :])
-                    terms.append(product[:, j, t, :])
-                    for i, term in enumerate(terms):
-                        nc.tensor.matmul(
-                            out=bank[:, t, :],
-                            lhsT=term,
-                            rhs=ident[:],
-                            is_transpose=True,
-                            start=(i == 0),
-                            stop=(i == len(terms) - 1),
-                        )
+                bank = banks_pool.tile([P, PACK, B], F32, tag="bank")
                 banks.append(bank)
+            plain = SUM_ROUNDS <= r < SUM_ROUNDS + PLAIN_ROUNDS
+            if plain:
+                for j in range(PAIR):
+                    for t in range(PACK):
+                        nc.tensor.matmul(
+                            out=banks[j][:, t, :], lhsT=f_half[:, t, :], rhs=ident_half[:], start=(t == 0), stop=False
+                        )
+            for j in range(PAIR):
+                terms = [lr_term[:, r * PAIR + j, :, :]]
+                if r >= SUM_ROUNDS + PLAIN_ROUNDS:
+                    terms.append(f_term[:])
+                flip_terms(banks[j], terms, not plain, False)
             return banks
+
+        def close_banks(banks, product):
+            for j in range(PAIR):
+                flip_terms(banks[j], [product[:, j, :, :]], False, True)
 
         def round_off(r, banks):
             pre = shared.tile([P, PAIR, B, PACK], BF16, tag="slot%d" % ((r + SLOTS - 1) % SLOTS), align_bytes=64)
@@ -216,7 +234,7 @@ def tile_hetxlhead_pa_kernel(
                 its_rows = slice(j * B, (j + 1) * B)
                 for n0 in range(0, C, N_TILE):
                     its_classes = slice(n0, n0 + N_TILE)
-                    acc = sums.tile([P, N_TILE], F32, tag="acc")
+                    acc = banks_pool.tile([P, N_TILE], F32, tag="bank")
                     nc.tensor.matmul_mx(
                         out=acc[:],
                         lhsT=codes[:, its_rows].bitcast(FP8X4),
@@ -250,8 +268,11 @@ def tile_hetxlhead_pa_kernel(
         nc.vector.tensor_tensor(out=std_term[:], in0=by_t(ramp[:]), in1=by_t(tail[:]), op=ALU.add)
 
         products = {}
+        opened = {}
         pres = {}
         accs = {}
+        opened[0] = open_banks(0)
+        opened[1] = open_banks(1)
         for n in range(-2, ROUNDS + 1):
             if 0 <= n < ROUNDS:
                 codes, scales = quantise(pres[n])
@@ -260,9 +281,11 @@ def tile_hetxlhead_pa_kernel(
             if SUM_ROUNDS <= n + 4 < ROUNDS:
                 widen_lr(n + 4)
             if 0 <= n + 1 < ROUNDS:
-                banks = flip(n + 1, products[n + 1])
-                pres[n + 1] = round_off(n + 1, banks)
+                close_banks(opened[n + 1], products[n + 1])
+                pres[n + 1] = round_off(n + 1, opened[n + 1])
             if 0 <= n < ROUNDS:
                 accs[n] = multiply(codes, scales)
+            if 2 <= n + 2 < ROUNDS:
+                opened[n + 2] = open_banks(n + 2)
             if n >= 1:
                 finish(n - 1, accs[n - 1])

@@ -26,7 +26,6 @@ LOAD_TILES = 4
 SUM_ROUNDS = 3
 VECTOR_ROUNDS = 2
 SLOTS = 3
-PLAIN_ROUNDS = 11
 
 FLOPS = 2 * B * D * D + 2 * B * S * D * C
 
@@ -116,10 +115,8 @@ def tile_hetxlhead_pa_kernel(
         nc.vector.quantize_mx(
             out=f_codes[:].bitcast(FP8X4), scales=f_scales[:], in_=f_grouped[:].rearrange("p b t -> p (b t)")
         )
-        f_term = keep.tile([P, PACK, P], F32)
+        f_term = keep.tile([P, PACK, P], BF16)
         nc.scalar.copy(out=f_term[:], in_=by_t(f_sb[:]))
-        f_half = keep.tile([P, PACK, P], BF16)
-        nc.scalar.copy(out=f_half[:], in_=by_t(f_sb[:]))
 
         bdiag_ps = banks_pool.tile([P, D], F32, tag="bank")
         nc.tensor.matmul(out=bdiag_ps[:], lhsT=ones[:], rhs=bias_rows[:, 0:D], start=True, stop=True)
@@ -191,23 +188,24 @@ def tile_hetxlhead_pa_kernel(
                         stop=(closes and i == len(terms) - 1 and t == PACK - 1),
                     )
 
+        def added_late(r, j):
+            return r >= SUM_ROUNDS and r % 2 == 1 and j == PAIR - 1
+
         def open_banks(r):
             banks = []
+            plain = []
             for j in range(PAIR):
                 bank = banks_pool.tile([P, PACK, B], F32, tag="bank")
                 banks.append(bank)
-            plain = SUM_ROUNDS <= r < SUM_ROUNDS + PLAIN_ROUNDS
-            if plain:
-                for j in range(PAIR):
+                plain.append(r >= SUM_ROUNDS and not added_late(r, j))
+            for j in range(PAIR):
+                if plain[j]:
                     for t in range(PACK):
                         nc.tensor.matmul(
-                            out=banks[j][:, t, :], lhsT=f_half[:, t, :], rhs=ident_half[:], start=(t == 0), stop=False
+                            out=banks[j][:, t, :], lhsT=f_term[:, t, :], rhs=ident_half[:], start=(t == 0), stop=False
                         )
             for j in range(PAIR):
-                terms = [lr_term[:, r * PAIR + j, :, :]]
-                if r >= SUM_ROUNDS + PLAIN_ROUNDS:
-                    terms.append(f_term[:])
-                flip_terms(banks[j], terms, not plain, False)
+                flip_terms(banks[j], [lr_term[:, r * PAIR + j, :, :]], not plain[j], False)
             return banks
 
         def close_banks(banks, product):
@@ -217,8 +215,16 @@ def tile_hetxlhead_pa_kernel(
         def round_off(r, banks):
             pre = shared.tile([P, PAIR, B, PACK], BF16, tag="slot%d" % ((r + SLOTS - 1) % SLOTS), align_bytes=64)
             for j in range(PAIR):
-                nc.scalar.copy(out=pre[:, j, :, :], in_=banks[j][:].rearrange("p t b -> p b t"))
+                if not added_late(r, j):
+                    nc.scalar.copy(out=pre[:, j, :, :], in_=banks[j][:].rearrange("p t b -> p b t"))
             return pre
+
+        def add_late(r, banks, pre):
+            for j in range(PAIR):
+                if added_late(r, j):
+                    nc.vector.tensor_tensor(
+                        out=pre[:, j, :, :], in0=banks[j][:].rearrange("p t b -> p b t"), in1=f_grouped[:], op=ALU.add
+                    )
 
         def quantise(pre):
             codes = work.tile([P, PAIR * B], U32, align_bytes=64)
@@ -247,20 +253,19 @@ def tile_hetxlhead_pa_kernel(
                     parts.append((j, its_classes, acc))
             return parts
 
-        def finish(r, parts):
-            for j in range(PAIR):
-                logits = store.tile([P, C], F32)
-                for its_j, its_classes, acc in parts:
-                    if its_j == j:
-                        nc.vector.scalar_tensor_tensor(
-                            out=logits[:, its_classes],
-                            in0=acc[:],
-                            scalar=INV_TEMPERATURE,
-                            in1=bias_scaled[:, its_classes],
-                            op0=ALU.mult,
-                            op1=ALU.add,
-                        )
-                nc.sync.dma_start(out=out[:, r * PAIR + j, :], in_=logits[:])
+        def finish(r, j, parts):
+            logits = store.tile([P, C], F32)
+            for its_j, its_classes, acc in parts:
+                if its_j == j:
+                    nc.vector.scalar_tensor_tensor(
+                        out=logits[:, its_classes],
+                        in0=acc[:],
+                        scalar=INV_TEMPERATURE,
+                        in1=bias_scaled[:, its_classes],
+                        op0=ALU.mult,
+                        op1=ALU.add,
+                    )
+            nc.sync.dma_start(out=out[:, r * PAIR + j, :], in_=logits[:])
 
         for r in range(SUM_ROUNDS):
             sum_lr(r)
@@ -288,4 +293,8 @@ def tile_hetxlhead_pa_kernel(
             if 2 <= n + 2 < ROUNDS:
                 opened[n + 2] = open_banks(n + 2)
             if n >= 1:
-                finish(n - 1, accs[n - 1])
+                finish(n - 1, 0, accs[n - 1])
+            if 0 <= n + 1 < ROUNDS:
+                add_late(n + 1, opened[n + 1], pres[n + 1])
+            if n >= 1:
+                finish(n - 1, 1, accs[n - 1])

@@ -23,7 +23,8 @@ N_TILE = 512
 PAIR = 2
 ROUNDS = S // PAIR
 LOAD_TILES = 4
-SUM_ROUNDS = 3
+SUM_ROUNDS = 4
+EARLY_SUMS = 3
 VECTOR_ROUNDS = 2
 SLOTS = 3
 
@@ -189,7 +190,7 @@ def tile_hetxlhead_pa_kernel(
                     )
 
         def added_late(r, j):
-            return r >= SUM_ROUNDS and r % 2 == 1 and j == PAIR - 1
+            return r >= SUM_ROUNDS and r % 4 == 1 and j == PAIR - 1
 
         def open_banks(r):
             banks = []
@@ -267,7 +268,7 @@ def tile_hetxlhead_pa_kernel(
                     )
             nc.sync.dma_start(out=out[:, r * PAIR + j, :], in_=logits[:])
 
-        for r in range(SUM_ROUNDS):
+        for r in range(EARLY_SUMS):
             sum_lr(r)
         std_term = keep.tile([P, PACK, P], F32)
         nc.vector.tensor_tensor(out=std_term[:], in0=by_t(ramp[:]), in1=by_t(tail[:]), op=ALU.add)
@@ -283,6 +284,9 @@ def tile_hetxlhead_pa_kernel(
                 codes, scales = quantise(pres[n])
             if 0 <= n + 2 < ROUNDS:
                 products[n + 2] = scale_noise(n + 2)
+            if n + 2 == VECTOR_ROUNDS - 1:
+                for r in range(EARLY_SUMS, SUM_ROUNDS):
+                    sum_lr(r)
             if SUM_ROUNDS <= n + 4 < ROUNDS:
                 widen_lr(n + 4)
             if 0 <= n + 1 < ROUNDS:

@@ -190,7 +190,7 @@ def tile_hetxlhead_pa_kernel(
                     )
 
         def added_late(r, j):
-            return r >= SUM_ROUNDS and r % 4 == 1 and j == PAIR - 1
+            return r >= SUM_ROUNDS and r % 2 == 1 and j == PAIR - 1
 
         def open_banks(r):
             banks = []
@@ -280,6 +280,8 @@ def tile_hetxlhead_pa_kernel(
         opened[0] = open_banks(0)
         opened[1] = open_banks(1)
         for n in range(-2, ROUNDS + 1):
+            if n >= 1:
+                finish(n - 1, 0, accs[n - 1])
             if 0 <= n < ROUNDS:
                 codes, scales = quantise(pres[n])
             if 0 <= n + 2 < ROUNDS:
@@ -297,8 +299,6 @@ def tile_hetxlhead_pa_kernel(
             if 2 <= n + 2 < ROUNDS:
                 opened[n + 2] = open_banks(n + 2)
             if n >= 1:
-                finish(n - 1, 0, accs[n - 1])
+                finish(n - 1, 1, accs[n - 1])
             if 0 <= n + 1 < ROUNDS:
                 add_late(n + 1, opened[n + 1], pres[n + 1])
-            if n >= 1:
-                finish(n - 1, 1, accs[n - 1])

@@ -23,10 +23,10 @@ N_TILE = 512
 PAIR = 2
 ROUNDS = S // PAIR
 LOAD_TILES = 4
-SUM_ROUNDS = 4
-EARLY_SUMS = 3
-VECTOR_ROUNDS = 2
-SLOTS = 3
+SUM_ROUNDS = 3
+AHEAD = 3
+VECTOR_ROUNDS = AHEAD
+SLOTS = AHEAD + 1
 
 FLOPS = 2 * B * D * D + 2 * B * S * D * C
 
@@ -268,7 +268,7 @@ def tile_hetxlhead_pa_kernel(
                     )
             nc.sync.dma_start(out=out[:, r * PAIR + j, :], in_=logits[:])
 
-        for r in range(EARLY_SUMS):
+        for r in range(SUM_ROUNDS):
             sum_lr(r)
         std_term = keep.tile([P, PACK, P], F32)
         nc.vector.tensor_tensor(out=std_term[:], in0=by_t(ramp[:]), in1=by_t(tail[:]), op=ALU.add)
@@ -279,16 +279,13 @@ def tile_hetxlhead_pa_kernel(
         accs = {}
         opened[0] = open_banks(0)
         opened[1] = open_banks(1)
-        for n in range(-2, ROUNDS + 1):
+        for n in range(-AHEAD, ROUNDS + 1):
             if n >= 1:
                 finish(n - 1, 0, accs[n - 1])
             if 0 <= n < ROUNDS:
                 codes, scales = quantise(pres[n])
-            if 0 <= n + 2 < ROUNDS:
-                products[n + 2] = scale_noise(n + 2)
-            if n + 2 == VECTOR_ROUNDS - 1:
-                for r in range(EARLY_SUMS, SUM_ROUNDS):
-                    sum_lr(r)
+            if n + AHEAD < ROUNDS:
+                products[n + AHEAD] = scale_noise(n + AHEAD)
             if SUM_ROUNDS <= n + 4 < ROUNDS:
                 widen_lr(n + 4)
             if 0 <= n + 1 < ROUNDS:

@@ -51,7 +51,7 @@ def tile_hetxlhead_pa_kernel(
         keep = stack.enter_context(tc.tile_pool(name="keep", bufs=1))
         shared = stack.enter_context(tc.tile_pool(name="shared", bufs=1))
         work = stack.enter_context(tc.tile_pool(name="work", bufs=3))
-        store = stack.enter_context(tc.tile_pool(name="store", bufs=6))
+        store = stack.enter_context(tc.tile_pool(name="store", bufs=12))
         banks_pool = stack.enter_context(tc.psum_pool(name="banks", bufs=8))
         stack.enter_context(tc.manual_schedule())
 

@@ -118,6 +118,8 @@ def tile_hetxlhead_pa_kernel(
         )
         f_term = keep.tile([P, PACK, P], BF16)
         nc.scalar.copy(out=f_term[:], in_=by_t(f_sb[:]))
+        f_flipped = keep.tile([P, PACK, B], BF16)
+        nc.scalar.copy(out=f_flipped[:], in_=f_grouped[:].rearrange("p b t -> p t b"))
 
         bdiag_ps = banks_pool.tile([P, D], F32, tag="bank")
         nc.tensor.matmul(out=bdiag_ps[:], lhsT=ones[:], rhs=bias_rows[:, 0:D], start=True, stop=True)
@@ -201,10 +203,13 @@ def tile_hetxlhead_pa_kernel(
                 plain.append(r >= SUM_ROUNDS and not added_late(r, j))
             for j in range(PAIR):
                 if plain[j]:
-                    for t in range(PACK):
-                        nc.tensor.matmul(
-                            out=banks[j][:, t, :], lhsT=f_term[:, t, :], rhs=ident_half[:], start=(t == 0), stop=False
-                        )
+                    nc.tensor.matmul(
+                        out=banks[j][:].rearrange("p t b -> p (t b)"),
+                        lhsT=ident_half[:],
+                        rhs=f_flipped[:].rearrange("p t b -> p (t b)"),
+                        start=True,
+                        stop=False,
+                    )
             for j in range(PAIR):
                 flip_terms(banks[j], [lr_term[:, r * PAIR + j, :, :]], not plain[j], False)
             return banks

@@ -32,7 +32,6 @@ FLOPS = 2 * B * D * D + 2 * B * S * D * C
 
 
 def load_weight(nc, words, plane, words_dram, scales_dram):
-    nc.vector.memset(plane[:].bitcast(I32), 0)
     scale_rows = scales_dram.rearrange("g q n -> (g q) n").bitcast(I32)
     for r in range(4):
         nc.sync.dma_start(out=plane[r:P:32, :].bitcast(I32), in_=scale_rows[r:16:4, :])
@@ -57,18 +56,23 @@ def tile_hetxlhead_pa_kernel(
 
         f_sb = keep.tile([P, D], BF16)
         nc.sync.dma_start(out=f_sb[:], in_=features)
-        bias_rows = keep.tile([P, D + C], BF16)
-        nc.vector.memset(bias_rows[:].bitcast(I32), 0)
-        nc.sync.dma_start(out=bias_rows[0:1, 0:D], in_=b_diag.unsqueeze(0))
-        nc.sync.dma_start(out=bias_rows[0:1, D : D + C], in_=b_cls.unsqueeze(0))
         wd_words = keep.tile([P, D], U32, align_bytes=64)
         wd_plane = keep.tile([P, D], U8, align_bytes=64)
+        nc.vector.memset(wd_plane[:].bitcast(I32), 0)
+        bdiag_rows = keep.tile([P, D], BF16)
+        nc.vector.memset(bdiag_rows[:].bitcast(I32), 0)
         load_weight(nc, wd_words, wd_plane, W_diag_words, W_diag_scales)
+        nc.sync.dma_start(out=bdiag_rows[0:1, :], in_=b_diag.unsqueeze(0))
+        ident = keep.tile([P, P], F32)
+        make_identity(nc, ident[:])
+        bcls_rows = keep.tile([P, C], BF16)
+        nc.gpsimd.memset(bcls_rows[:].bitcast(I32), 0)
 
         noise_sb = keep.tile([P, S, D], BF16)
         lr_sb = keep.tile([P, S, D], BF16)
         wc_words = keep.tile([P, C], U32, align_bytes=64)
         wc_plane = keep.tile([P, C], U8, align_bytes=64)
+        nc.gpsimd.memset(wc_plane[:].bitcast(I32), 0)
 
         def load_tiles(dst, src, first):
             some = slice(first, first + LOAD_TILES)
@@ -76,6 +80,7 @@ def tile_hetxlhead_pa_kernel(
 
         load_tiles(lr_sb, lr_samples, 0)
         load_tiles(lr_sb, lr_samples, LOAD_TILES)
+        nc.sync.dma_start(out=bcls_rows[0:1, :], in_=b_cls.unsqueeze(0))
         load_tiles(noise_sb, noise_diag, 0)
         load_weight(nc, wc_words, wc_plane, W_cls_words, W_cls_scales)
         load_tiles(noise_sb, noise_diag, LOAD_TILES)
@@ -83,8 +88,6 @@ def tile_hetxlhead_pa_kernel(
             load_tiles(lr_sb, lr_samples, first)
             load_tiles(noise_sb, noise_diag, first)
 
-        ident = keep.tile([P, P], F32)
-        make_identity(nc, ident[:])
         ident_half = keep.tile([P, P], BF16)
         make_identity(nc, ident_half[:])
         ones = keep.tile([P, P], BF16)
@@ -122,7 +125,7 @@ def tile_hetxlhead_pa_kernel(
         nc.scalar.copy(out=f_flipped[:], in_=f_grouped[:].rearrange("p b t -> p t b"))
 
         bdiag_ps = banks_pool.tile([P, D], F32, tag="bank")
-        nc.tensor.matmul(out=bdiag_ps[:], lhsT=ones[:], rhs=bias_rows[:, 0:D], start=True, stop=True)
+        nc.tensor.matmul(out=bdiag_ps[:], lhsT=ones[:], rhs=bdiag_rows[:], start=True, stop=True)
         bdiag_all = keep.tile([P, D], F32)
         nc.scalar.copy(out=bdiag_all[:], in_=bdiag_ps[:])
 
@@ -136,20 +139,31 @@ def tile_hetxlhead_pa_kernel(
             start=True,
             stop=True,
         )
+        halves = [slice(h * (D // 2), (h + 1) * (D // 2)) for h in range(2)]
         z = keep.tile([P, D], F32)
-        nc.vector.tensor_tensor(out=z[:], in0=z_ps[:], in1=bdiag_all[:], op=ALU.add)
         tail = keep.tile([P, D], F32)
-        nc.scalar.activation(out=tail[:], in_=z[:], func=ACT.Abs)
-        nc.scalar.activation(out=tail[:], in_=tail[:], func=ACT.Exp, scale=-1.0)
-        nc.scalar.activation(out=tail[:], in_=tail[:], func=ACT.Ln, bias=one[:])
-        ramp = keep.tile([P, D], F32)
-        nc.vector.tensor_scalar(out=ramp[:], in0=z[:], scalar1=0.0, scalar2=MIN_SCALE, op0=ALU.max, op1=ALU.add)
+        for half in halves:
+            nc.vector.tensor_tensor(out=z[:, half], in0=z_ps[:, half], in1=bdiag_all[:, half], op=ALU.add)
+        nc.vector.scalar_tensor_tensor(
+            out=tail[:, halves[1]], in0=z[:, halves[1]], scalar=-1.0, in1=z[:, halves[1]], op0=ALU.mult, op1=ALU.max
+        )
+        nc.scalar.activation(out=tail[:, halves[0]], in_=z[:, halves[0]], func=ACT.Abs)
+        for half in halves:
+            nc.scalar.activation(out=tail[:, half], in_=tail[:, half], func=ACT.Exp, scale=-1.0)
+        t_halves = [slice(0, PACK // 2), slice(PACK // 2, PACK)]
+        tail_term = keep.tile([P, PACK, P], F32)
+        for half in t_halves:
+            nc.scalar.activation(out=tail_term[:, half, :], in_=by_t(tail[:])[:, half, :], func=ACT.Ln, bias=one[:])
+        ramp_term = keep.tile([P, PACK, P], F32)
+        nc.vector.tensor_scalar(
+            out=ramp_term[:], in0=by_t(z[:]), scalar1=0.0, scalar2=MIN_SCALE, op0=ALU.max, op1=ALU.add
+        )
 
         bias_scaled = keep.tile([P, C], F32)
         for n0 in range(0, C, N_TILE):
             bcls_ps = banks_pool.tile([P, N_TILE], F32, tag="bank")
             nc.tensor.matmul(
-                out=bcls_ps[:], lhsT=ones[:], rhs=bias_rows[:, D + n0 : D + n0 + N_TILE], start=True, stop=True
+                out=bcls_ps[:], lhsT=ones[:], rhs=bcls_rows[:, n0 : n0 + N_TILE], start=True, stop=True
             )
             nc.scalar.mul(out=bias_scaled[:, n0 : n0 + N_TILE], in_=bcls_ps[:], mul=INV_TEMPERATURE)
 
@@ -166,17 +180,23 @@ def tile_hetxlhead_pa_kernel(
         def widen_lr(r):
             nc.scalar.copy(out=lr_term[:, its_tiles(r), :, :], in_=by_t(lr_sb[:, its_tiles(r), :]))
 
-        def scale_noise(r):
+        def product_slot(r):
             product = shared.tile([P, PAIR, PACK, P], F32, tag="slot%d" % (r % SLOTS), align_bytes=64)
-            if r < VECTOR_ROUNDS:
-                for j in range(PAIR):
-                    nc.vector.tensor_tensor(
-                        out=product[:, j, :, :], in0=by_t(noise_sb[:, r * PAIR + j, :]), in1=std_term[:], op=ALU.mult
-                    )
-            else:
-                nc.gpsimd.tensor_tensor(
-                    out=product[:], in0=by_t(noise_sb[:, its_tiles(r), :]), in1=for_pair(std_term[:]), op=ALU.mult
-                )
+            return product
+
+        def scale_tile(r, j, product, some_t=slice(0, PACK)):
+            nc.vector.tensor_tensor(
+                out=product[:, j, some_t, :],
+                in0=by_t(noise_sb[:, its_tiles(r), :])[:, j, some_t, :],
+                in1=std_term[:, some_t, :],
+                op=ALU.mult,
+            )
+
+        def scale_round(r):
+            product = product_slot(r)
+            nc.gpsimd.tensor_tensor(
+                out=product[:], in0=by_t(noise_sb[:, its_tiles(r), :]), in1=for_pair(std_term[:]), op=ALU.mult
+            )
             return product
 
         def flip_terms(bank, terms, opens, closes):
@@ -232,13 +252,18 @@ def tile_hetxlhead_pa_kernel(
                         out=pre[:, j, :, :], in0=banks[j][:].rearrange("p t b -> p b t"), in1=f_grouped[:], op=ALU.add
                     )
 
-        def quantise(pre):
+        def code_tiles():
             codes = work.tile([P, PAIR * B], U32, align_bytes=64)
             scales = work.tile([P, PAIR * B], U8, align_bytes=64)
-            nc.vector.quantize_mx(
-                out=codes[:].bitcast(FP8X4), scales=scales[:], in_=pre[:].rearrange("p j b t -> p (j b t)")
-            )
             return codes, scales
+
+        def quantise(pre, codes, scales, first=0, last=PAIR):
+            rows = slice(first * B, last * B)
+            nc.vector.quantize_mx(
+                out=codes[:, rows].bitcast(FP8X4),
+                scales=scales[:, rows],
+                in_=pre[:, first:last, :, :].rearrange("p j b t -> p (j b t)"),
+            )
 
         def multiply(codes, scales):
             parts = []
@@ -276,7 +301,10 @@ def tile_hetxlhead_pa_kernel(
         for r in range(SUM_ROUNDS):
             sum_lr(r)
         std_term = keep.tile([P, PACK, P], F32)
-        nc.vector.tensor_tensor(out=std_term[:], in0=by_t(ramp[:]), in1=by_t(tail[:]), op=ALU.add)
+        for half in t_halves:
+            nc.vector.tensor_tensor(
+                out=std_term[:, half, :], in0=ramp_term[:, half, :], in1=tail_term[:, half, :], op=ALU.add
+            )
 
         products = {}
         opened = {}
@@ -284,23 +312,41 @@ def tile_hetxlhead_pa_kernel(
         accs = {}
         opened[0] = open_banks(0)
         opened[1] = open_banks(1)
-        for n in range(-AHEAD, ROUNDS + 1):
+
+        for r in range(VECTOR_ROUNDS):
+            products[r] = product_slot(r)
+        for half in t_halves:
+            scale_tile(0, 0, products[0], half)
+        scale_tile(0, 1, products[0])
+        for j in range(PAIR):
+            scale_tile(1, j, products[1])
+        if SUM_ROUNDS < 4:
+            widen_lr(SUM_ROUNDS)
+        close_banks(opened[0], products[0])
+        pres[0] = round_off(0, opened[0])
+        codes, scales = code_tiles()
+        for j in range(PAIR):
+            scale_tile(2, j, products[2])
+            quantise(pres[0], codes, scales, j, j + 1)
+
+        for n in range(ROUNDS + 1):
             if n >= 1:
                 finish(n - 1, 0, accs[n - 1])
-            if 0 <= n < ROUNDS:
-                codes, scales = quantise(pres[n])
+            if 1 <= n < ROUNDS:
+                codes, scales = code_tiles()
+                quantise(pres[n], codes, scales)
             if n + AHEAD < ROUNDS:
-                products[n + AHEAD] = scale_noise(n + AHEAD)
-            if SUM_ROUNDS <= n + 4 < ROUNDS:
+                products[n + AHEAD] = scale_round(n + AHEAD)
+            if n + 4 < ROUNDS:
                 widen_lr(n + 4)
-            if 0 <= n + 1 < ROUNDS:
+            if n + 1 < ROUNDS:
                 close_banks(opened[n + 1], products[n + 1])
                 pres[n + 1] = round_off(n + 1, opened[n + 1])
-            if 0 <= n < ROUNDS:
+            if n < ROUNDS:
                 accs[n] = multiply(codes, scales)
-            if 2 <= n + 2 < ROUNDS:
+            if n + 2 < ROUNDS:
                 opened[n + 2] = open_banks(n + 2)
             if n >= 1:
                 finish(n - 1, 1, accs[n - 1])
-            if 0 <= n + 1 < ROUNDS:
+            if n + 1 < ROUNDS:
                 add_late(n + 1, opened[n + 1], pres[n + 1])

@@ -23,7 +23,8 @@ N_TILE = 512
 PAIR = 2
 ROUNDS = S // PAIR
 LOAD_TILES = 4
-SUM_ROUNDS = 3
+SUM_ROUNDS = range(1, 3)
+LAST_SUM = S // PAIR - 1
 AHEAD = 3
 VECTOR_ROUNDS = AHEAD
 SLOTS = AHEAD + 1
@@ -74,16 +75,17 @@ def tile_hetxlhead_pa_kernel(
         wc_plane = keep.tile([P, C], U8, align_bytes=64)
         nc.gpsimd.memset(wc_plane[:].bitcast(I32), 0)
 
-        def load_tiles(dst, src, first):
-            some = slice(first, first + LOAD_TILES)
+        def load_tiles(dst, src, first, count=LOAD_TILES):
+            some = slice(first, first + count)
             nc.sync.dma_start(out=dst[:, some, :], in_=src[:, some, :])
 
         load_tiles(lr_sb, lr_samples, 0)
-        load_tiles(lr_sb, lr_samples, LOAD_TILES)
-        nc.sync.dma_start(out=bcls_rows[0:1, :], in_=b_cls.unsqueeze(0))
+        load_tiles(lr_sb, lr_samples, LOAD_TILES, PAIR)
         load_tiles(noise_sb, noise_diag, 0)
+        nc.sync.dma_start(out=bcls_rows[0:1, :], in_=b_cls.unsqueeze(0))
         load_weight(nc, wc_words, wc_plane, W_cls_words, W_cls_scales)
         load_tiles(noise_sb, noise_diag, LOAD_TILES)
+        load_tiles(lr_sb, lr_samples, LOAD_TILES + PAIR, PAIR)
         for first in range(2 * LOAD_TILES, S, LOAD_TILES):
             load_tiles(lr_sb, lr_samples, first)
             load_tiles(noise_sb, noise_diag, first)
@@ -139,6 +141,13 @@ def tile_hetxlhead_pa_kernel(
             start=True,
             stop=True,
         )
+        bcls_banks = []
+        for n0 in range(0, C, N_TILE):
+            bcls_ps = banks_pool.tile([P, N_TILE], F32, tag="bank")
+            nc.tensor.matmul(
+                out=bcls_ps[:], lhsT=ones[:], rhs=bcls_rows[:, n0 : n0 + N_TILE], start=True, stop=True
+            )
+            bcls_banks.append(bcls_ps)
         halves = [slice(h * (D // 2), (h + 1) * (D // 2)) for h in range(2)]
         z = keep.tile([P, D], F32)
         tail = keep.tile([P, D], F32)
@@ -159,26 +168,21 @@ def tile_hetxlhead_pa_kernel(
             out=ramp_term[:], in0=by_t(z[:]), scalar1=0.0, scalar2=MIN_SCALE, op0=ALU.max, op1=ALU.add
         )
 
-        bias_scaled = keep.tile([P, C], F32)
-        for n0 in range(0, C, N_TILE):
-            bcls_ps = banks_pool.tile([P, N_TILE], F32, tag="bank")
-            nc.tensor.matmul(
-                out=bcls_ps[:], lhsT=ones[:], rhs=bcls_rows[:, n0 : n0 + N_TILE], start=True, stop=True
-            )
-            nc.scalar.mul(out=bias_scaled[:, n0 : n0 + N_TILE], in_=bcls_ps[:], mul=INV_TEMPERATURE)
-
         lr_term = keep.tile([P, S, PACK, P], F32)
 
         def its_tiles(r):
             return slice(r * PAIR, (r + 1) * PAIR)
 
-        def sum_lr(r):
-            nc.vector.tensor_tensor(
+        def summed(r):
+            return r in SUM_ROUNDS or r == LAST_SUM
+
+        def sum_lr(engine, r):
+            engine.tensor_tensor(
                 out=lr_term[:, its_tiles(r), :, :], in0=by_t(lr_sb[:, its_tiles(r), :]), in1=for_pair(f_term[:]), op=ALU.add
             )
 
-        def widen_lr(r):
-            nc.scalar.copy(out=lr_term[:, its_tiles(r), :, :], in_=by_t(lr_sb[:, its_tiles(r), :]))
+        def widen_lr(tiles):
+            nc.scalar.copy(out=lr_term[:, tiles, :, :], in_=by_t(lr_sb[:, tiles, :]))
 
         def product_slot(r):
             product = shared.tile([P, PAIR, PACK, P], F32, tag="slot%d" % (r % SLOTS), align_bytes=64)
@@ -212,15 +216,17 @@ def tile_hetxlhead_pa_kernel(
                     )
 
         def added_late(r, j):
-            return r >= SUM_ROUNDS and r % 2 == 1 and j == PAIR - 1
+            return not summed(r) and r % 2 == 1 and j == PAIR - 1
 
-        def open_banks(r):
+        def two_banks():
             banks = []
-            plain = []
             for j in range(PAIR):
                 bank = banks_pool.tile([P, PACK, B], F32, tag="bank")
                 banks.append(bank)
-                plain.append(r >= SUM_ROUNDS and not added_late(r, j))
+            return banks
+
+        def open_banks(r, banks):
+            plain = [not summed(r) and not added_late(r, j) for j in range(PAIR)]
             for j in range(PAIR):
                 if plain[j]:
                     nc.tensor.matmul(
@@ -232,7 +238,6 @@ def tile_hetxlhead_pa_kernel(
                     )
             for j in range(PAIR):
                 flip_terms(banks[j], [lr_term[:, r * PAIR + j, :, :]], not plain[j], False)
-            return banks
 
         def close_banks(banks, product):
             for j in range(PAIR):
@@ -298,8 +303,8 @@ def tile_hetxlhead_pa_kernel(
                     )
             nc.sync.dma_start(out=out[:, r * PAIR + j, :], in_=logits[:])
 
-        for r in range(SUM_ROUNDS):
-            sum_lr(r)
+        for r in SUM_ROUNDS:
+            sum_lr(nc.vector, r)
         std_term = keep.tile([P, PACK, P], F32)
         for half in t_halves:
             nc.vector.tensor_tensor(
@@ -310,8 +315,16 @@ def tile_hetxlhead_pa_kernel(
         opened = {}
         pres = {}
         accs = {}
-        opened[0] = open_banks(0)
-        opened[1] = open_banks(1)
+        for j in range(PAIR):
+            widen_lr(slice(j, j + 1))
+        for r in range(2):
+            opened[r] = two_banks()
+        for r in (1, 0):
+            open_banks(r, opened[r])
+
+        bias_scaled = keep.tile([P, C], F32)
+        for h, bcls_ps in enumerate(bcls_banks):
+            nc.scalar.mul(out=bias_scaled[:, h * N_TILE : (h + 1) * N_TILE], in_=bcls_ps[:], mul=INV_TEMPERATURE)
 
         for r in range(VECTOR_ROUNDS):
             products[r] = product_slot(r)
@@ -320,8 +333,6 @@ def tile_hetxlhead_pa_kernel(
         scale_tile(0, 1, products[0])
         for j in range(PAIR):
             scale_tile(1, j, products[1])
-        if SUM_ROUNDS < 4:
-            widen_lr(SUM_ROUNDS)
         close_banks(opened[0], products[0])
         pres[0] = round_off(0, opened[0])
         codes, scales = code_tiles()
@@ -337,15 +348,18 @@ def tile_hetxlhead_pa_kernel(
                 quantise(pres[n], codes, scales)
             if n + AHEAD < ROUNDS:
                 products[n + AHEAD] = scale_round(n + AHEAD)
-            if n + 4 < ROUNDS:
-                widen_lr(n + 4)
+            if n + AHEAD == ROUNDS - 1:
+                sum_lr(nc.gpsimd, LAST_SUM)
             if n + 1 < ROUNDS:
                 close_banks(opened[n + 1], products[n + 1])
                 pres[n + 1] = round_off(n + 1, opened[n + 1])
+            if n + 3 < ROUNDS and not summed(n + 3):
+                widen_lr(its_tiles(n + 3))
             if n < ROUNDS:
                 accs[n] = multiply(codes, scales)
             if n + 2 < ROUNDS:
-                opened[n + 2] = open_banks(n + 2)
+                opened[n + 2] = two_banks()
+                open_banks(n + 2, opened[n + 2])
             if n >= 1:
                 finish(n - 1, 1, accs[n - 1])
             if n + 1 < ROUNDS:

@@ -52,7 +52,7 @@ def tile_hetxlhead_pa_kernel(
         shared = stack.enter_context(tc.tile_pool(name="shared", bufs=1))
         work = stack.enter_context(tc.tile_pool(name="work", bufs=3))
         store = stack.enter_context(tc.tile_pool(name="store", bufs=12))
-        banks_pool = stack.enter_context(tc.psum_pool(name="banks", bufs=8))
+        banks_pool = stack.enter_context(tc.psum_pool(name="banks", bufs=1))
         stack.enter_context(tc.manual_schedule())
 
         f_sb = keep.tile([P, D], BF16)
@@ -99,6 +99,9 @@ def tile_hetxlhead_pa_kernel(
         warm = keep.tile([P, 1], F32)
         nc.scalar.activation(out=warm[:], in_=one[:], func=ACT.Exp)
 
+        def bank_tag(pair, i):
+            return "bank%d" % (2 * pair + i)
+
         def by_t(rows):
             if rows.ndim == 2:
                 return rows.rearrange("b (p t) -> b t p", t=PACK)
@@ -107,7 +110,7 @@ def tile_hetxlhead_pa_kernel(
         def for_pair(row):
             return row.unsqueeze(1).to_broadcast([P, PAIR, PACK, P])
 
-        fT_ps = banks_pool.tile([P, HALVES, B], F32, tag="bank")
+        fT_ps = banks_pool.tile([P, HALVES, B], F32, tag=bank_tag(3, 0))
         f_words = f_sb[:].bitcast(F32)
         for u in range(HALVES):
             nc.tensor.transpose(out=fT_ps[:, u, :], in_=f_words[:, u : D // 2 : HALVES], identity=ident[:])
@@ -126,12 +129,12 @@ def tile_hetxlhead_pa_kernel(
         f_flipped = keep.tile([P, PACK, B], BF16)
         nc.scalar.copy(out=f_flipped[:], in_=f_grouped[:].rearrange("p b t -> p t b"))
 
-        bdiag_ps = banks_pool.tile([P, D], F32, tag="bank")
+        bdiag_ps = banks_pool.tile([P, D], F32, tag=bank_tag(3, 1))
         nc.tensor.matmul(out=bdiag_ps[:], lhsT=ones[:], rhs=bdiag_rows[:], start=True, stop=True)
         bdiag_all = keep.tile([P, D], F32)
         nc.scalar.copy(out=bdiag_all[:], in_=bdiag_ps[:])
 
-        z_ps = banks_pool.tile([P, D], F32, tag="bank")
+        z_ps = banks_pool.tile([P, D], F32, tag=bank_tag(2, 0))
         nc.tensor.matmul_mx(
             out=z_ps[:],
             lhsT=f_codes[:].bitcast(FP8X4),
@@ -142,11 +145,10 @@ def tile_hetxlhead_pa_kernel(
             stop=True,
         )
         bcls_banks = []
-        for n0 in range(0, C, N_TILE):
-            bcls_ps = banks_pool.tile([P, N_TILE], F32, tag="bank")
-            nc.tensor.matmul(
-                out=bcls_ps[:], lhsT=ones[:], rhs=bcls_rows[:, n0 : n0 + N_TILE], start=True, stop=True
-            )
+        for h in range(C // N_TILE):
+            its_classes = slice(h * N_TILE, (h + 1) * N_TILE)
+            bcls_ps = banks_pool.tile([P, N_TILE], F32, tag=bank_tag(3, h))
+            nc.tensor.matmul(out=bcls_ps[:], lhsT=ones[:], rhs=bcls_rows[:, its_classes], start=True, stop=True)
             bcls_banks.append(bcls_ps)
         halves = [slice(h * (D // 2), (h + 1) * (D // 2)) for h in range(2)]
         z = keep.tile([P, D], F32)
@@ -218,10 +220,10 @@ def tile_hetxlhead_pa_kernel(
         def added_late(r, j):
             return not summed(r) and r % 2 == 1 and j == PAIR - 1
 
-        def two_banks():
+        def two_banks(pair):
             banks = []
             for j in range(PAIR):
-                bank = banks_pool.tile([P, PACK, B], F32, tag="bank")
+                bank = banks_pool.tile([P, PACK, B], F32, tag=bank_tag(pair, j))
                 banks.append(bank)
             return banks
 
@@ -270,13 +272,13 @@ def tile_hetxlhead_pa_kernel(
                 in_=pre[:, first:last, :, :].rearrange("p j b t -> p (j b t)"),
             )
 
-        def multiply(codes, scales):
+        def multiply(codes, scales, pairs):
             parts = []
             for j in range(PAIR):
                 its_rows = slice(j * B, (j + 1) * B)
-                for n0 in range(0, C, N_TILE):
-                    its_classes = slice(n0, n0 + N_TILE)
-                    acc = banks_pool.tile([P, N_TILE], F32, tag="bank")
+                for h in range(C // N_TILE):
+                    its_classes = slice(h * N_TILE, (h + 1) * N_TILE)
+                    acc = banks_pool.tile([P, N_TILE], F32, tag=bank_tag(pairs[j], h))
                     nc.tensor.matmul_mx(
                         out=acc[:],
                         lhsT=codes[:, its_rows].bitcast(FP8X4),
@@ -301,7 +303,10 @@ def tile_hetxlhead_pa_kernel(
                         op0=ALU.mult,
                         op1=ALU.add,
                     )
-            nc.sync.dma_start(out=out[:, r * PAIR + j, :], in_=logits[:])
+                    if r * PAIR + j == S - 1:
+                        nc.sync.dma_start(out=out[:, S - 1, its_classes], in_=logits[:, its_classes])
+            if r * PAIR + j < S - 1:
+                nc.sync.dma_start(out=out[:, r * PAIR + j, :], in_=logits[:])
 
         for r in SUM_ROUNDS:
             sum_lr(nc.vector, r)
@@ -317,9 +322,10 @@ def tile_hetxlhead_pa_kernel(
         accs = {}
         for j in range(PAIR):
             widen_lr(slice(j, j + 1))
-        for r in range(2):
-            opened[r] = two_banks()
-        for r in (1, 0):
+        opening_pairs = {r: r for r in range(3)}
+        for r in range(3):
+            opened[r] = two_banks(opening_pairs[r])
+        for r in (1, 2, 0):
             open_banks(r, opened[r])
 
         bias_scaled = keep.tile([P, C], F32)
@@ -340,12 +346,17 @@ def tile_hetxlhead_pa_kernel(
             scale_tile(2, j, products[2])
             quantise(pres[0], codes, scales, j, j + 1)
 
+        pairs = [3, opening_pairs[0]]
         for n in range(ROUNDS + 1):
             if n >= 1:
                 finish(n - 1, 0, accs[n - 1])
             if 1 <= n < ROUNDS:
                 codes, scales = code_tiles()
-                quantise(pres[n], codes, scales)
+                if n == ROUNDS - 1:
+                    for j in range(PAIR):
+                        quantise(pres[n], codes, scales, j, j + 1)
+                else:
+                    quantise(pres[n], codes, scales)
             if n + AHEAD < ROUNDS:
                 products[n + AHEAD] = scale_round(n + AHEAD)
             if n + AHEAD == ROUNDS - 1:
@@ -356,10 +367,14 @@ def tile_hetxlhead_pa_kernel(
             if n + 3 < ROUNDS and not summed(n + 3):
                 widen_lr(its_tiles(n + 3))
             if n < ROUNDS:
-                accs[n] = multiply(codes, scales)
-            if n + 2 < ROUNDS:
-                opened[n + 2] = two_banks()
+                accs[n] = multiply(codes, scales, pairs)
+            if 1 <= n and n + 2 < ROUNDS:
+                opening_pairs[n + 2] = before[1]
+                opened[n + 2] = two_banks(before[1])
                 open_banks(n + 2, opened[n + 2])
+            if n + 1 < ROUNDS:
+                before = pairs
+                pairs = [opening_pairs[n + 1], before[0]]
             if n >= 1:
                 finish(n - 1, 1, accs[n - 1])
             if n + 1 < ROUNDS:

@@ -24,7 +24,6 @@ PAIR = 2
 ROUNDS = S // PAIR
 LOAD_TILES = 4
 SUM_ROUNDS = range(1, 3)
-LAST_SUM = S // PAIR - 1
 AHEAD = 3
 VECTOR_ROUNDS = AHEAD
 SLOTS = AHEAD + 1
@@ -176,10 +175,10 @@ def tile_hetxlhead_pa_kernel(
             return slice(r * PAIR, (r + 1) * PAIR)
 
         def summed(r):
-            return r in SUM_ROUNDS or r == LAST_SUM
+            return r in SUM_ROUNDS
 
-        def sum_lr(engine, r):
-            engine.tensor_tensor(
+        def sum_lr(r):
+            nc.vector.tensor_tensor(
                 out=lr_term[:, its_tiles(r), :, :], in0=by_t(lr_sb[:, its_tiles(r), :]), in1=for_pair(f_term[:]), op=ALU.add
             )
 
@@ -309,7 +308,7 @@ def tile_hetxlhead_pa_kernel(
                 nc.sync.dma_start(out=out[:, r * PAIR + j, :], in_=logits[:])
 
         for r in SUM_ROUNDS:
-            sum_lr(nc.vector, r)
+            sum_lr(r)
         std_term = keep.tile([P, PACK, P], F32)
         for half in t_halves:
             nc.vector.tensor_tensor(
@@ -359,8 +358,6 @@ def tile_hetxlhead_pa_kernel(
                     quantise(pres[n], codes, scales)
             if n + AHEAD < ROUNDS:
                 products[n + AHEAD] = scale_round(n + AHEAD)
-            if n + AHEAD == ROUNDS - 1:
-                sum_lr(nc.gpsimd, LAST_SUM)
             if n + 1 < ROUNDS:
                 close_banks(opened[n + 1], products[n + 1])
                 pres[n + 1] = round_off(n + 1, opened[n + 1])

@@ -125,6 +125,7 @@ def tile_hetxlhead_pa_kernel(
         )
         f_term = keep.tile([P, PACK, P], BF16)
         nc.scalar.copy(out=f_term[:], in_=by_t(f_sb[:]))
+        f_wide = keep.tile([P, PACK, P], F32)
         f_flipped = keep.tile([P, PACK, B], BF16)
         nc.scalar.copy(out=f_flipped[:], in_=f_grouped[:].rearrange("p b t -> p t b"))
 
@@ -216,8 +217,11 @@ def tile_hetxlhead_pa_kernel(
                         stop=(closes and i == len(terms) - 1 and t == PACK - 1),
                     )
 
+        def transposed_features(r, j):
+            return not summed(r) and r % 4 == 3 and j == PAIR - 1 and r < ROUNDS - 1
+
         def added_late(r, j):
-            return not summed(r) and r % 2 == 1 and j == PAIR - 1
+            return not summed(r) and r % 4 == 1 and j == PAIR - 1
 
         def two_banks(pair):
             banks = []
@@ -227,7 +231,9 @@ def tile_hetxlhead_pa_kernel(
             return banks
 
         def open_banks(r, banks):
-            plain = [not summed(r) and not added_late(r, j) for j in range(PAIR)]
+            plain = [
+                not (summed(r) or transposed_features(r, j) or added_late(r, j)) for j in range(PAIR)
+            ]
             for j in range(PAIR):
                 if plain[j]:
                     nc.tensor.matmul(
@@ -238,7 +244,10 @@ def tile_hetxlhead_pa_kernel(
                         stop=False,
                     )
             for j in range(PAIR):
-                flip_terms(banks[j], [lr_term[:, r * PAIR + j, :, :]], not plain[j], False)
+                terms = [lr_term[:, r * PAIR + j, :, :]]
+                if transposed_features(r, j):
+                    terms.append(f_wide)
+                flip_terms(banks[j], terms, not plain[j], False)
 
         def close_banks(banks, product):
             for j in range(PAIR):
@@ -327,6 +336,7 @@ def tile_hetxlhead_pa_kernel(
         for r in (1, 2, 0):
             open_banks(r, opened[r])
 
+        nc.scalar.copy(out=f_wide[:], in_=f_term[:])
         bias_scaled = keep.tile([P, C], F32)
         for h, bcls_ps in enumerate(bcls_banks):
             nc.scalar.mul(out=bias_scaled[:, h * N_TILE : (h + 1) * N_TILE], in_=bcls_ps[:], mul=INV_TEMPERATURE)

@@ -26,6 +26,7 @@ LOAD_TILES = 4
 SUM_ROUNDS = range(1, 3)
 AHEAD = 3
 VECTOR_ROUNDS = AHEAD
+VECTOR_SHARE = 16
 SLOTS = AHEAD + 1
 
 FLOPS = 2 * B * D * D + 2 * B * S * D * C
@@ -200,9 +201,13 @@ def tile_hetxlhead_pa_kernel(
 
         def scale_round(r):
             product = product_slot(r)
-            nc.gpsimd.tensor_tensor(
-                out=product[:], in0=by_t(noise_sb[:, its_tiles(r), :]), in1=for_pair(std_term[:]), op=ALU.mult
-            )
+            for engine, some_p in ((nc.vector, slice(P - VECTOR_SHARE, P)), (nc.gpsimd, slice(0, P - VECTOR_SHARE))):
+                engine.tensor_tensor(
+                    out=product[:, :, :, some_p],
+                    in0=by_t(noise_sb[:, its_tiles(r), :])[:, :, :, some_p],
+                    in1=for_pair(std_term[:])[:, :, :, some_p],
+                    op=ALU.mult,
+                )
             return product
 
         def flip_terms(bank, terms, opens, closes):

from contextlib import ExitStack

import concourse.mybir as mybir
from concourse.masks import make_identity

F32 = mybir.dt.float32
BF16 = mybir.dt.bfloat16
I32 = mybir.dt.int32
U32 = mybir.dt.uint32
U8 = mybir.dt.uint8
FP8X4 = mybir.dt.float8_e4m3fn_x4
ACT = mybir.ActivationFunctionType
ALU = mybir.AluOpType

B, S, D, C = 128, 32, 512, 1024
MIN_SCALE = 1e-3
INV_TEMPERATURE = 1.0 / 1.5

P = 128
PACK = 4
HALVES = 2
N_TILE = 512
PAIR = 2
ROUNDS = S // PAIR
LOAD_TILES = 4
SUM_ROUNDS = range(1, 3)
AHEAD = 3
VECTOR_ROUNDS = AHEAD
VECTOR_SHARE = 16
SLOTS = AHEAD + 1

FLOPS = 2 * B * D * D + 2 * B * S * D * C


def load_weight(nc, words, plane, words_dram, scales_dram):
    scale_rows = scales_dram.rearrange("g q n -> (g q) n").bitcast(I32)
    for r in range(4):
        nc.sync.dma_start(out=plane[r:P:32, :].bitcast(I32), in_=scale_rows[r:16:4, :])
    nc.sync.dma_start(
        out=words[:].bitcast(I32),
        in_=words_dram.rearrange("g p n t -> (g p) (n t)").bitcast(I32),
    )


def tile_hetxlhead_pa_kernel(
    tc, features, W_diag_words, W_diag_scales, b_diag, W_cls_words, W_cls_scales, b_cls, noise_diag, lr_samples, out
):
    nc = tc.nc

    with ExitStack() as stack:
        keep = stack.enter_context(tc.tile_pool(name="keep", bufs=1))
        shared = stack.enter_context(tc.tile_pool(name="shared", bufs=1))
        work = stack.enter_context(tc.tile_pool(name="work", bufs=3))
        store = stack.enter_context(tc.tile_pool(name="store", bufs=12))
        banks_pool = stack.enter_context(tc.psum_pool(name="banks", bufs=1))
        stack.enter_context(tc.manual_schedule())

        f_sb = keep.tile([P, D], BF16)
        nc.sync.dma_start(out=f_sb[:], in_=features)
        wd_words = keep.tile([P, D], U32, align_bytes=64)
        wd_plane = keep.tile([P, D], U8, align_bytes=64)
        nc.vector.memset(wd_plane[:].bitcast(I32), 0)
        bdiag_rows = keep.tile([P, D], BF16)
        nc.vector.memset(bdiag_rows[:].bitcast(I32), 0)
        load_weight(nc, wd_words, wd_plane, W_diag_words, W_diag_scales)
        nc.sync.dma_start(out=bdiag_rows[0:1, :], in_=b_diag.unsqueeze(0))
        ident = keep.tile([P, P], F32)
        make_identity(nc, ident[:])
        bcls_rows = keep.tile([P, C], BF16)
        nc.gpsimd.memset(bcls_rows[:].bitcast(I32), 0)

        noise_sb = keep.tile([P, S, D], BF16)
        lr_sb = keep.tile([P, S, D], BF16)
        wc_words = keep.tile([P, C], U32, align_bytes=64)
        wc_plane = keep.tile([P, C], U8, align_bytes=64)
        nc.gpsimd.memset(wc_plane[:].bitcast(I32), 0)

        def load_tiles(dst, src, first, count=LOAD_TILES):
            some = slice(first, first + count)
            nc.sync.dma_start(out=dst[:, some, :], in_=src[:, some, :])

        load_tiles(lr_sb, lr_samples, 0)
        load_tiles(lr_sb, lr_samples, LOAD_TILES, PAIR)
        load_tiles(noise_sb, noise_diag, 0)
        nc.sync.dma_start(out=bcls_rows[0:1, :], in_=b_cls.unsqueeze(0))
        load_weight(nc, wc_words, wc_plane, W_cls_words, W_cls_scales)
        load_tiles(noise_sb, noise_diag, LOAD_TILES)
        load_tiles(lr_sb, lr_samples, LOAD_TILES + PAIR, PAIR)
        for first in range(2 * LOAD_TILES, S, LOAD_TILES):
            load_tiles(lr_sb, lr_samples, first)
            load_tiles(noise_sb, noise_diag, first)

        ident_half = keep.tile([P, P], BF16)
        make_identity(nc, ident_half[:])
        ones = keep.tile([P, P], BF16)
        nc.vector.memset(ones[:], 1.0)
        one = keep.tile([P, 1], F32)
        nc.vector.memset(one[:], 1.0)
        warm = keep.tile([P, 1], F32)
        nc.scalar.activation(out=warm[:], in_=one[:], func=ACT.Exp)

        def bank_tag(pair, i):
            return "bank%d" % (2 * pair + i)

        def by_t(rows):
            if rows.ndim == 2:
                return rows.rearrange("b (p t) -> b t p", t=PACK)
            return rows.rearrange("b s (p t) -> b s t p", t=PACK)

        def for_pair(row):
            return row.unsqueeze(1).to_broadcast([P, PAIR, PACK, P])

        fT_ps = banks_pool.tile([P, HALVES, B], F32, tag=bank_tag(3, 0))
        f_words = f_sb[:].bitcast(F32)
        for u in range(HALVES):
            nc.tensor.transpose(out=fT_ps[:, u, :], in_=f_words[:, u : D // 2 : HALVES], identity=ident[:])
        f_grouped = keep.tile([P, B, PACK], BF16, align_bytes=64)
        nc.vector.tensor_copy(
            out=f_grouped[:].rearrange("p b t -> p (b t)").bitcast(F32).rearrange("p (b u) -> p b u", u=HALVES),
            in_=fT_ps[:].rearrange("p u b -> p b u"),
        )
        f_codes = keep.tile([P, B], U32, align_bytes=64)
        f_scales = keep.tile([P, B], U8, align_bytes=64)
        nc.vector.quantize_mx(
            out=f_codes[:].bitcast(FP8X4), scales=f_scales[:], in_=f_grouped[:].rearrange("p b t -> p (b t)")
        )
        f_term = keep.tile([P, PACK, P], BF16)
        nc.scalar.copy(out=f_term[:], in_=by_t(f_sb[:]))
        f_wide = keep.tile([P, PACK, P], F32)
        f_flipped = keep.tile([P, PACK, B], BF16)
        nc.scalar.copy(out=f_flipped[:], in_=f_grouped[:].rearrange("p b t -> p t b"))

        bdiag_ps = banks_pool.tile([P, D], F32, tag=bank_tag(3, 1))
        nc.tensor.matmul(out=bdiag_ps[:], lhsT=ones[:], rhs=bdiag_rows[:], start=True, stop=True)
        bdiag_all = keep.tile([P, D], F32)
        nc.scalar.copy(out=bdiag_all[:], in_=bdiag_ps[:])

        z_ps = banks_pool.tile([P, D], F32, tag=bank_tag(2, 0))
        nc.tensor.matmul_mx(
            out=z_ps[:],
            lhsT=f_codes[:].bitcast(FP8X4),
            lhsT_scale=f_scales[:],
            rhs=wd_words[:].bitcast(FP8X4),
            rhs_scale=wd_plane[:],
            start=True,
            stop=True,
        )
        bcls_banks = []
        for h in range(C // N_TILE):
            its_classes = slice(h * N_TILE, (h + 1) * N_TILE)
            bcls_ps = banks_pool.tile([P, N_TILE], F32, tag=bank_tag(3, h))
            nc.tensor.matmul(out=bcls_ps[:], lhsT=ones[:], rhs=bcls_rows[:, its_classes], start=True, stop=True)
            bcls_banks.append(bcls_ps)
        halves = [slice(h * (D // 2), (h + 1) * (D // 2)) for h in range(2)]
        z = keep.tile([P, D], F32)
        tail = keep.tile([P, D], F32)
        for half in halves:
            nc.vector.tensor_tensor(out=z[:, half], in0=z_ps[:, half], in1=bdiag_all[:, half], op=ALU.add)
        nc.vector.scalar_tensor_tensor(
            out=tail[:, halves[1]], in0=z[:, halves[1]], scalar=-1.0, in1=z[:, halves[1]], op0=ALU.mult, op1=ALU.max
        )
        nc.scalar.activation(out=tail[:, halves[0]], in_=z[:, halves[0]], func=ACT.Abs)
        for half in halves:
            nc.scalar.activation(out=tail[:, half], in_=tail[:, half], func=ACT.Exp, scale=-1.0)
        t_halves = [slice(0, PACK // 2), slice(PACK // 2, PACK)]
        tail_term = keep.tile([P, PACK, P], F32)
        for half in t_halves:
            nc.scalar.activation(out=tail_term[:, half, :], in_=by_t(tail[:])[:, half, :], func=ACT.Ln, bias=one[:])
        ramp_term = keep.tile([P, PACK, P], F32)
        nc.vector.tensor_scalar(
            out=ramp_term[:], in0=by_t(z[:]), scalar1=0.0, scalar2=MIN_SCALE, op0=ALU.max, op1=ALU.add
        )

        lr_term = keep.tile([P, S, PACK, P], F32)

        def its_tiles(r):
            return slice(r * PAIR, (r + 1) * PAIR)

        def summed(r):
            return r in SUM_ROUNDS

        def sum_lr(r):
            nc.vector.tensor_tensor(
                out=lr_term[:, its_tiles(r), :, :], in0=by_t(lr_sb[:, its_tiles(r), :]), in1=for_pair(f_term[:]), op=ALU.add
            )

        def widen_lr(tiles):
            nc.scalar.copy(out=lr_term[:, tiles, :, :], in_=by_t(lr_sb[:, tiles, :]))

        def product_slot(r):
            product = shared.tile([P, PAIR, PACK, P], F32, tag="slot%d" % (r % SLOTS), align_bytes=64)
            return product

        def scale_tile(r, j, product, some_t=slice(0, PACK)):
            nc.vector.tensor_tensor(
                out=product[:, j, some_t, :],
                in0=by_t(noise_sb[:, its_tiles(r), :])[:, j, some_t, :],
                in1=std_term[:, some_t, :],
                op=ALU.mult,
            )

        def scale_round(r):
            product = product_slot(r)
            for engine, some_p in ((nc.vector, slice(P - VECTOR_SHARE, P)), (nc.gpsimd, slice(0, P - VECTOR_SHARE))):
                engine.tensor_tensor(
                    out=product[:, :, :, some_p],
                    in0=by_t(noise_sb[:, its_tiles(r), :])[:, :, :, some_p],
                    in1=for_pair(std_term[:])[:, :, :, some_p],
                    op=ALU.mult,
                )
            return product

        def flip_terms(bank, terms, opens, closes):
            for i, term in enumerate(terms):
                for t in range(PACK):
                    nc.tensor.matmul(
                        out=bank[:, t, :],
                        lhsT=term[:, t, :],
                        rhs=ident[:],
                        is_transpose=True,
                        start=(opens and i == 0 and t == 0),
                        stop=(closes and i == len(terms) - 1 and t == PACK - 1),
                    )

        def transposed_features(r, j):
            return not summed(r) and r % 4 == 3 and j == PAIR - 1 and r < ROUNDS - 1

        def added_late(r, j):
            return not summed(r) and r % 4 == 1 and j == PAIR - 1

        def two_banks(pair):
            banks = []
            for j in range(PAIR):
                bank = banks_pool.tile([P, PACK, B], F32, tag=bank_tag(pair, j))
                banks.append(bank)
            return banks

        def open_banks(r, banks):
            plain = [
                not (summed(r) or transposed_features(r, j) or added_late(r, j)) for j in range(PAIR)
            ]
            for j in range(PAIR):
                if plain[j]:
                    nc.tensor.matmul(
                        out=banks[j][:].rearrange("p t b -> p (t b)"),
                        lhsT=ident_half[:],
                        rhs=f_flipped[:].rearrange("p t b -> p (t b)"),
                        start=True,
                        stop=False,
                    )
            for j in range(PAIR):
                terms = [lr_term[:, r * PAIR + j, :, :]]
                if transposed_features(r, j):
                    terms.append(f_wide)
                flip_terms(banks[j], terms, not plain[j], False)

        def close_banks(banks, product):
            for j in range(PAIR):
                flip_terms(banks[j], [product[:, j, :, :]], False, True)

        def round_off(r, banks):
            pre = shared.tile([P, PAIR, B, PACK], BF16, tag="slot%d" % ((r + SLOTS - 1) % SLOTS), align_bytes=64)
            for j in range(PAIR):
                if not added_late(r, j):
                    nc.scalar.copy(out=pre[:, j, :, :], in_=banks[j][:].rearrange("p t b -> p b t"))
            return pre

        def add_late(r, banks, pre):
            for j in range(PAIR):
                if added_late(r, j):
                    nc.vector.tensor_tensor(
                        out=pre[:, j, :, :], in0=banks[j][:].rearrange("p t b -> p b t"), in1=f_grouped[:], op=ALU.add
                    )

        def code_tiles():
            codes = work.tile([P, PAIR * B], U32, align_bytes=64)
            scales = work.tile([P, PAIR * B], U8, align_bytes=64)
            return codes, scales

        def quantise(pre, codes, scales, first=0, last=PAIR):
            rows = slice(first * B, last * B)
            nc.vector.quantize_mx(
                out=codes[:, rows].bitcast(FP8X4),
                scales=scales[:, rows],
                in_=pre[:, first:last, :, :].rearrange("p j b t -> p (j b t)"),
            )

        def multiply(codes, scales, pairs):
            parts = []
            for j in range(PAIR):
                its_rows = slice(j * B, (j + 1) * B)
                for h in range(C // N_TILE):
                    its_classes = slice(h * N_TILE, (h + 1) * N_TILE)
                    acc = banks_pool.tile([P, N_TILE], F32, tag=bank_tag(pairs[j], h))
                    nc.tensor.matmul_mx(
                        out=acc[:],
                        lhsT=codes[:, its_rows].bitcast(FP8X4),
                        lhsT_scale=scales[:, its_rows],
                        rhs=wc_words[:, its_classes].bitcast(FP8X4),
                        rhs_scale=wc_plane[:, its_classes],
                        start=True,
                        stop=True,
                    )
                    parts.append((j, its_classes, acc))
            return parts

        def finish(r, j, parts):
            logits = store.tile([P, C], F32)
            for its_j, its_classes, acc in parts:
                if its_j == j:
                    nc.vector.scalar_tensor_tensor(
                        out=logits[:, its_classes],
                        in0=acc[:],
                        scalar=INV_TEMPERATURE,
                        in1=bias_scaled[:, its_classes],
                        op0=ALU.mult,
                        op1=ALU.add,
                    )
                    if r * PAIR + j == S - 1:
                        nc.sync.dma_start(out=out[:, S - 1, its_classes], in_=logits[:, its_classes])
            if r * PAIR + j < S - 1:
                nc.sync.dma_start(out=out[:, r * PAIR + j, :], in_=logits[:])

        for r in SUM_ROUNDS:
            sum_lr(r)
        std_term = keep.tile([P, PACK, P], F32)
        for half in t_halves:
            nc.vector.tensor_tensor(
                out=std_term[:, half, :], in0=ramp_term[:, half, :], in1=tail_term[:, half, :], op=ALU.add
            )

        products = {}
        opened = {}
        pres = {}
        accs = {}
        for j in range(PAIR):
            widen_lr(slice(j, j + 1))
        opening_pairs = {r: r for r in range(3)}
        for r in range(3):
            opened[r] = two_banks(opening_pairs[r])
        for r in (1, 2, 0):
            open_banks(r, opened[r])

        nc.scalar.copy(out=f_wide[:], in_=f_term[:])
        bias_scaled = keep.tile([P, C], F32)
        for h, bcls_ps in enumerate(bcls_banks):
            nc.scalar.mul(out=bias_scaled[:, h * N_TILE : (h + 1) * N_TILE], in_=bcls_ps[:], mul=INV_TEMPERATURE)

        for r in range(VECTOR_ROUNDS):
            products[r] = product_slot(r)
        for half in t_halves:
            scale_tile(0, 0, products[0], half)
        scale_tile(0, 1, products[0])
        for j in range(PAIR):
            scale_tile(1, j, products[1])
        close_banks(opened[0], products[0])
        pres[0] = round_off(0, opened[0])
        codes, scales = code_tiles()
        for j in range(PAIR):
            scale_tile(2, j, products[2])
            quantise(pres[0], codes, scales, j, j + 1)

        pairs = [3, opening_pairs[0]]
        for n in range(ROUNDS + 1):
            if n >= 1:
                finish(n - 1, 0, accs[n - 1])
            if 1 <= n < ROUNDS:
                codes, scales = code_tiles()
                if n == ROUNDS - 1:
                    for j in range(PAIR):
                        quantise(pres[n], codes, scales, j, j + 1)
                else:
                    quantise(pres[n], codes, scales)
            if n + AHEAD < ROUNDS:
                products[n + AHEAD] = scale_round(n + AHEAD)
            if n + 1 < ROUNDS:
                close_banks(opened[n + 1], products[n + 1])
                pres[n + 1] = round_off(n + 1, opened[n + 1])
            if n + 3 < ROUNDS and not summed(n + 3):
                widen_lr(its_tiles(n + 3))
            if n < ROUNDS:
                accs[n] = multiply(codes, scales, pairs)
            if 1 <= n and n + 2 < ROUNDS:
                opening_pairs[n + 2] = before[1]
                opened[n + 2] = two_banks(before[1])
                open_banks(n + 2, opened[n + 2])
            if n + 1 < ROUNDS:
                before = pairs
                pairs = [opening_pairs[n + 1], before[0]]
            if n >= 1:
                finish(n - 1, 1, accs[n - 1])
            if n + 1 < ROUNDS:
                add_late(n + 1, opened[n + 1], pres[n + 1])
